import numpy as np
import ml_dtypes


def mxq(x, axis, fmt="e4m3"):
    dtype, down = {"e4m3": (ml_dtypes.float8_e4m3fn, 7), "e5m2": (ml_dtypes.float8_e5m2, 14)}[fmt]
    v = np.moveaxis(np.asarray(x, np.float32).astype(ml_dtypes.bfloat16).astype(np.float64), axis, -1)
    blocks = v.reshape(v.shape[:-1] + (-1, 32))
    amax = np.abs(blocks).max(-1, keepdims=True)
    byte = np.maximum(np.where(amax > 0, np.frexp(amax)[1] - 1 + 127, 0) - down, 1)
    scale = np.exp2(byte - 127.0)
    codes = (blocks / scale).astype(np.float32).astype(dtype).astype(np.float64)
    return np.moveaxis((codes * scale).reshape(v.shape), -1, axis)


WIDE = False


def mx_kscale(k):
    if not WIDE:
        return np.ones(k)
    levels = np.array([10, -10, 5, -5, 0])
    a = np.random.permutation(np.resize(levels, k // 512 * 4)).reshape(k // 512, 4)
    idx = np.arange(k)
    return np.exp2(a[idx // 512, idx % 128 // 32])


BF16 = ml_dtypes.bfloat16


def bf(x):
    return np.asarray(x, np.float32).astype(BF16)


def f64(x):
    return np.asarray(x).astype(np.float64)


E2M1 = np.array([0.0, 0.5, 1.0, 1.5, 2.0, 3.0, 4.0, 6.0, -0.0, -0.5, -1.0, -1.5, -2.0, -3.0, -4.0, -6.0])


def pack_weight(w, fmt):
    k, n = w.shape
    w = f64(bf(w)).reshape(k // 32, 32, n)
    amax = np.abs(w).max(1)
    if fmt == "e4m3":
        byte = np.frexp(amax)[1] - 1 + 127 - 7
    else:
        mant, ex = np.frexp(amax / 6.0)
        byte = np.where(mant > 0.5, ex, ex - 1) + 127
    byte = np.clip(np.where(amax > 0, byte, 1), 1, 254)
    scaled = (w * np.exp2(127.0 - byte)[:, None, :]).reshape(k, n).astype(np.float32)
    by_word = np.ascontiguousarray(scaled.reshape(k // 512, 128, 4, n).transpose(0, 1, 3, 2))
    if fmt == "e4m3":
        words = by_word.astype(ml_dtypes.float8_e4m3fn).view(np.uint8)
    else:
        c = by_word.astype(ml_dtypes.float4_e2m1fn).view(np.uint8) & 0xF
        words = c[..., 0::2] | (c[..., 1::2] << 4)
    return np.ascontiguousarray(words), np.ascontiguousarray(byte.astype(np.uint8).reshape(k // 512, 16, n))


def unpack_weight(words, scales, fmt):
    g, p, n, _ = words.shape
    if fmt == "e4m3":
        vals = np.ascontiguousarray(words).view(ml_dtypes.float8_e4m3fn).astype(np.float64)
    else:
        nib = np.empty((g, p, n, 4), np.uint8)
        nib[..., 0::2] = words & 0xF
        nib[..., 1::2] = words >> 4
        vals = E2M1[nib]
    vals = vals * np.repeat(np.exp2(scales.astype(np.float64) - 127.0), 8, axis=1)[..., None]
    return vals.transpose(0, 1, 3, 2).reshape(g * 512, n)

def pack4(w):
    words, scales = pack_weight(w, "e2m1")
    return words.reshape(words.shape[0], 128, -1), scales


def unpack4(words, scales):
    return unpack_weight(words.reshape(words.shape[0], 128, -1, 2), scales, "e2m1")


B, N, C0, C1, C2, O0, O1, O2 = 256, 16, 256, 512, 128, 512, 256, 512
P = C0 + C1
K = P + 2 * C2


def sigmoid(v):
    return 1.0 / (1.0 + np.exp(-v))


def setup_inputs():
    s = mx_kscale(K)[:P]
    lo = 0.4 * np.random.random((B, N, 1, C2))
    hi = 1.0 - 0.4 * np.random.random((B, N, 1, C2))
    x2 = lo + (hi - lo) * np.random.random((B, N, N, C2))
    i = np.arange(N)
    x2[:, i, i, :] = np.random.random((B, N, C2)) < 0.5
    w = np.random.standard_normal((K, O1)) * 2.0 / np.sqrt(K)
    w[:P] = w[:P] / s[:, None]
    words, scales = pack4(w)
    return {"x0": bf(np.random.random((B, C0)) * s[:C0]),
            "x1": bf(np.random.random((B, N, C1)) * s[C0:]),
            "x2": bf(x2),
            "W1_words": words,
            "W1_scales": scales,
            "b1": bf(np.random.standard_normal(O1) * 0.3)}


def reference(x0, x1, x2, W1_words, W1_scales, b1):
    x0, x1, x2 = f64(x0), f64(x1), f64(x2)
    e0 = np.broadcast_to(x0[:, None, :], (B, N, C0))
    diag = np.eye(N, dtype=bool)[None, :, :, None]
    rmax = np.where(diag, 0.0, x2).max(axis=2)
    rmin = np.where(diag, 1.0, x2).min(axis=2)
    f1 = np.concatenate([e0, x1, rmax, rmin], axis=-1)
    return sigmoid((mxq(f1, 2, "e4m3") @ unpack4(W1_words, W1_scales)) + f64(b1))

@@ -1,0 +1,283 @@
+from contextlib import ExitStack
+
+import concourse.mybir as mybir
+from concourse.masks import make_identity
+
+BF16 = mybir.dt.bfloat16
+F32 = mybir.dt.float32
+I32 = mybir.dt.int32
+U8 = mybir.dt.uint8
+U32 = mybir.dt.uint32
+FP8X4 = mybir.dt.float8_e4m3fn_x4
+FP4X4 = mybir.dt.float4_e2m1fn_x4
+ALU = mybir.AluOpType
+ACT = mybir.ActivationFunctionType
+
+P = 128
+SCENES, OBJECTS, C0, C1, C2, OUT = 256, 16, 256, 512, 128, 256
+K = C0 + C1 + 2 * C2
+HALVES = SCENES // P
+PARTNERS = OBJECTS - 1
+RUN = OBJECTS * C2
+RUNS = OBJECTS - 1
+CHUNK = 4
+CHUNKS_PER_HALF = OBJECTS // CHUNK
+N_CHUNKS = HALVES * CHUNKS_PER_HALF
+PAIRS = CHUNK // 2
+OUT_HALVES = OUT // P
+
+FLOPS = 2 * SCENES * OBJECTS * K * OUT
+BYTES = (
+    2 * (SCENES * C0 + SCENES * OBJECTS * C1 + SCENES * OBJECTS * PARTNERS * C2 + OUT)
+    + K * OUT // 2
+    + K * OUT // 32
+    + 4 * SCENES * OBJECTS * OUT
+)
+
+
+def tile_differentiablelogicmachine_pb_t_kernel(tc, x0, x1, x2, W1_words, W1_scales, b1, out):
+    nc = tc.nc
+    with ExitStack() as ctx:
+        const = ctx.enter_context(tc.tile_pool(name="const", bufs=1))
+        x2_pool = ctx.enter_context(tc.tile_pool(name="x2", bufs=HALVES))
+        x1_pool = ctx.enter_context(tc.tile_pool(name="x1", bufs=3))
+        tree_pool = ctx.enter_context(tc.tile_pool(name="tree", bufs=2))
+        grouped_pool = ctx.enter_context(tc.tile_pool(name="grouped", bufs=2))
+        code_pool = ctx.enter_context(tc.tile_pool(name="codes", bufs=2))
+        out_pool = ctx.enter_context(tc.tile_pool(name="outs", bufs=2))
+        psum_in = ctx.enter_context(tc.psum_pool(name="psum_in", bufs=3))
+        psum_acc = ctx.enter_context(tc.psum_pool(name="psum_acc", bufs=2))
+        psum_out = ctx.enter_context(tc.psum_pool(name="psum_out", bufs=2))
+        ctx.enter_context(tc.manual_schedule())
+
+        x2_tiles = {}
+        x1_tiles = {}
+
+        def load_x2(chunk):
+            half, part = divmod(chunk, CHUNKS_PER_HALF)
+            if part == 0:
+                x2_sb = x2_pool.tile([P, RUNS, RUN], BF16)
+                x2_tiles[half] = x2_sb
+            table = x2[half * P : (half + 1) * P].rearrange("b i j c -> b (i j c)")
+            runs = table[:, C2:].rearrange("b (g r) -> b g r", r=RUN + C2)
+            g0, g1 = CHUNK * part, min(CHUNK * (part + 1), RUNS)
+            nc.sync.dma_start(out=x2_tiles[half][:, g0:g1, :], in_=runs[:, g0:g1, 0:RUN])
+
+        def load_x1(chunk):
+            half, part = divmod(chunk, CHUNKS_PER_HALF)
+            x1_sb = x1_pool.tile([P, CHUNK, C1], BF16)
+            x1_tiles[chunk] = x1_sb
+            nc.sync.dma_start(
+                out=x1_sb[:], in_=x1[half * P : (half + 1) * P, CHUNK * part : CHUNK * (part + 1), :]
+            )
+
+        load_x2(0)
+        load_x1(0)
+        x0_sb = const.tile([P, HALVES, C0], BF16)
+        nc.sync.dma_start(out=x0_sb[:], in_=x0.rearrange("(h b) k -> b h k", h=HALVES))
+        load_x2(1)
+        load_x1(1)
+
+        w_x1 = const.tile([P, 2 * OUT], U8, align_bytes=64)
+        w_low = const.tile([P, 2, 2 * OUT], U8, align_bytes=64)
+        w_high = const.tile([P, 2, 2 * OUT], U8, align_bytes=64)
+        s_x1 = const.tile([P, OUT], U8, align_bytes=64)
+        s_low = const.tile([P, 2, OUT], U8, align_bytes=64)
+        s_high = const.tile([P, 2, OUT], U8, align_bytes=64)
+        for zeroed in (w_low, w_high, s_x1, s_low, s_high):
+            nc.vector.memset(zeroed[:].bitcast(I32), 0)
+        bias_rows = const.tile([P, P], BF16)
+        nc.vector.memset(bias_rows[:], 0.0)
+        table_warmer = const.tile([P, 2], F32)
+        nc.vector.memset(table_warmer[:, 0:1], 0.0)
+        nc.scalar.activation(out=table_warmer[:, 1:2], in_=table_warmer[:, 0:1], func=ACT.Sigmoid)
+
+        ident_f32 = const.tile([P, P], F32)
+        make_identity(nc, ident_f32[:])
+        ident_bf16 = const.tile([P, P], BF16)
+        make_identity(nc, ident_bf16[:])
+
+        words_by_64 = W1_words.rearrange("g (s p) n -> p (g s) n", p=64)
+        nc.sync.dma_start(
+            out=w_x1[:].bitcast(I32), in_=W1_words.rearrange("g p n -> (g p) n")[64:192, :].bitcast(I32)
+        )
+        nc.sync.dma_start(out=w_low[0:64].bitcast(I32), in_=words_by_64[:, 0:4:3, :].bitcast(I32))
+        nc.sync.dma_start(out=w_high[64:128].bitcast(I32), in_=words_by_64[:, 0:4:3, :].bitcast(I32))
+        nc.sync.dma_start(out=bias_rows[0:OUT_HALVES, :], in_=b1.rearrange("(h o) -> h o", h=OUT_HALVES))
+        scales_by_8 = W1_scales.rearrange("g (s q) n -> q (g s) n", q=8)
+        scale_rows = W1_scales.rearrange("g q n -> (g q) n")
+        for quad in range(4):
+            nc.sync.dma_start(
+                out=s_x1[32 * quad : 32 * quad + 4, :].bitcast(I32),
+                in_=scale_rows[8 + 4 * quad : 12 + 4 * quad, :].bitcast(I32),
+            )
+        for quad in range(2):
+            rows = scales_by_8[4 * quad : 4 * quad + 4, 0:4:3, :].bitcast(I32)
+            nc.sync.dma_start(out=s_low[32 * quad : 32 * quad + 4].bitcast(I32), in_=rows)
+            nc.sync.dma_start(out=s_high[64 + 32 * quad : 64 + 32 * quad + 4].bitcast(I32), in_=rows)
+
+        def transpose_words(bank_part, words, first):
+            for u in range(2):
+                nc.tensor.transpose(bank_part[:, u, :], words[:, first + u : first + 2 * P : 2], ident_f32[:])
+
+        x0_grouped = const.tile([P, P, 4], BF16, align_bytes=64)
+        x0_codes = const.tile([P, P], U32, align_bytes=64)
+        x0_scales = const.tile([P, P], U8, align_bytes=64)
+        bias = const.tile([P, OUT_HALVES], F32)
+
+        def transpose_x0():
+            bank = psum_in.tile([P, 2, P], F32, tag="bank_in")
+            transpose_words(bank, x0_sb[:].rearrange("b h k -> b (h k)").bitcast(F32), 0)
+            nc.scalar.copy(out=x0_grouped[:].bitcast(F32), in_=bank[:].rearrange("p u b -> p b u"))
+
+        def transpose_bias():
+            bank = psum_in.tile([P, P], BF16, tag="bank_in")
+            nc.tensor.transpose(bank[:], bias_rows[:], ident_bf16[:])
+            nc.scalar.copy(out=bias[:], in_=bank[:, 0:OUT_HALVES])
+
+        trees = {}
+        r_tiles = {}
+        x1_grouped = {}
+        r_grouped = {}
+        x1_mx = {}
+        r_mx = {}
+
+        def partners_of(chunk):
+            half, part = divmod(chunk, CHUNKS_PER_HALF)
+            rows = x2_tiles[half][:].rearrange("b g r -> b (g r)").rearrange("b (i s c) -> b i s c", s=PARTNERS, c=C2)
+            return rows[:, CHUNK * part : CHUNK * (part + 1)]
+
+        def tree_first_level(chunk):
+            x = partners_of(chunk)
+            top = tree_pool.tile([P, CHUNK, 7, C2], BF16)
+            low = tree_pool.tile([P, CHUNK, 7, C2], BF16)
+            trees[chunk] = ((ALU.max, top), (ALU.min, low))
+            for op, t in trees[chunk]:
+                nc.vector.tensor_tensor(out=t[:, :, 0:7, :], in0=x[:, :, 0:7, :], in1=x[:, :, 7:14, :], op=op)
+
+        def tree_other_levels(chunk):
+            x = partners_of(chunk)
+            r = tree_pool.tile([P, CHUNK, 2, C2], BF16)
+            r_tiles[chunk] = r
+            for op, t in trees[chunk]:
+                nc.vector.tensor_tensor(out=t[:, :, 3:6, :], in0=t[:, :, 0:3, :], in1=t[:, :, 3:6, :], op=op)
+            for op, t in trees[chunk]:
+                nc.vector.tensor_tensor(out=t[:, :, 6, :], in0=t[:, :, 6, :], in1=x[:, :, 14, :], op=op)
+            for op, t in trees[chunk]:
+                nc.vector.tensor_tensor(out=t[:, :, 3:5, :], in0=t[:, :, 3:5, :], in1=t[:, :, 5:7, :], op=op)
+            for which, (op, t) in enumerate(trees[chunk]):
+                nc.vector.tensor_tensor(out=r[:, :, which, :], in0=t[:, :, 3, :], in1=t[:, :, 4, :], op=op)
+            nc.vector.tensor_scalar_max(out=r[:, :, 0, :], in0=r[:, :, 0, :], scalar1=0.0)
+            nc.vector.tensor_scalar_min(out=r[:, :, 1, :], in0=r[:, :, 1, :], scalar1=1.0)
+
+        def transpose_x1(chunk):
+            words = x1_tiles[chunk][:].rearrange("b a k -> b (a k)").bitcast(F32)
+            grouped = grouped_pool.tile([P, CHUNK, P, 4], BF16, align_bytes=64, tag="x1_grouped")
+            x1_grouped[chunk] = grouped
+            for pair in range(PAIRS):
+                bank = psum_in.tile([P, 2, 2, P], F32, tag="bank_in")
+                for j in range(2):
+                    transpose_words(bank[:, j], words, (2 * pair + j) * (C1 // 2))
+                nc.scalar.copy(
+                    out=grouped[:, 2 * pair : 2 * pair + 2].bitcast(F32), in_=bank[:].rearrange("p a u b -> p a b u")
+                )
+
+        def transpose_r(chunk):
+            words = r_tiles[chunk][:].rearrange("b a m c -> b (a m c)").bitcast(F32)
+            grouped = grouped_pool.tile([P, PAIRS, P, 4], BF16, align_bytes=64, tag="r_grouped")
+            r_grouped[chunk] = grouped
+            bank = psum_in.tile([P, PAIRS, 2, P], F32, tag="bank_in")
+            for pair in range(PAIRS):
+                transpose_words(bank[:, pair], words, pair * 2 * C2)
+            nc.scalar.copy(out=grouped[:].bitcast(F32), in_=bank[:].rearrange("p a u b -> p a b u"))
+
+        def quantise(grouped, columns, tag):
+            codes = code_pool.tile([P, columns, P], U32, align_bytes=64, tag=tag + "_codes")
+            scales = code_pool.tile([P, columns, P], U8, align_bytes=64, tag=tag + "_scales")
+            nc.vector.quantize_mx(
+                out=codes[:].rearrange("p a b -> p (a b)").bitcast(FP8X4),
+                scales=scales[:].rearrange("p a b -> p (a b)"),
+                in_=grouped[:].rearrange("p a b t -> p (a b t)"),
+            )
+            return codes, scales
+
+        def multiply(chunk):
+            half, part = divmod(chunk, CHUNKS_PER_HALF)
+            x1_codes, x1_scales = x1_mx[chunk]
+            r_codes, r_scales = r_mx[chunk]
+            w_x0, s_x0 = (w_low, s_low) if half == 0 else (w_high, s_high)
+            result = out_pool.tile([P, CHUNK, OUT], F32, tag="result")
+            sigmoids = []
+            for oh in range(OUT_HALVES):
+                w_cols = slice(2 * P * oh, 2 * P * (oh + 1))
+                s_cols = slice(P * oh, P * (oh + 1))
+                acc = psum_acc.tile([P, CHUNK, P], F32, tag="acc")
+                for a in range(CHUNK):
+                    pair, second = divmod(a, 2)
+                    w_r, s_r = (w_low, s_low) if second == 0 else (w_high, s_high)
+                    nc.tensor.matmul_mx(
+                        out=acc[:, a, :],
+                        lhsT=w_x1[:, w_cols].bitcast(FP4X4),
+                        lhsT_scale=s_x1[:, s_cols],
+                        rhs=x1_codes[:, a, :].bitcast(FP8X4),
+                        rhs_scale=x1_scales[:, a, :],
+                        start=True,
+                        stop=False,
+                    )
+                    nc.tensor.matmul_mx(
+                        out=acc[:, a, :],
+                        lhsT=w_x0[:, 0, w_cols].bitcast(FP4X4),
+                        lhsT_scale=s_x0[:, 0, s_cols],
+                        rhs=x0_codes[:].bitcast(FP8X4),
+                        rhs_scale=x0_scales[:],
+                        start=False,
+                        stop=False,
+                    )
+                    nc.tensor.matmul_mx(
+                        out=acc[:, a, :],
+                        lhsT=w_r[:, 1, w_cols].bitcast(FP4X4),
+                        lhsT_scale=s_r[:, 1, s_cols],
+                        rhs=r_codes[:, pair, :].bitcast(FP8X4),
+                        rhs_scale=r_scales[:, pair, :],
+                        start=False,
+                        stop=True,
+                    )
+                sig = out_pool.tile([P, CHUNK, P], F32, tag="sig")
+                nc.scalar.activation(out=sig[:], in_=acc[:], func=ACT.Sigmoid, bias=bias[:, oh : oh + 1], scale=1.0)
+                sigmoids.append(sig)
+            for oh in range(OUT_HALVES):
+                back = psum_out.tile([P, CHUNK, P], F32, tag="back")
+                for a in range(CHUNK):
+                    nc.tensor.transpose(back[:, a, :], sigmoids[oh][:, a, :], ident_f32[:])
+                nc.scalar.copy(out=result[:, :, P * oh : P * (oh + 1)], in_=back[:])
+            nc.sync.dma_start(
+                out=out[half * P : (half + 1) * P, CHUNK * part : CHUNK * (part + 1), :], in_=result[:]
+            )
+
+        transpose_x1(0)
+        transpose_x0()
+        for step in range(N_CHUNKS + 1):
+            now, before, ahead = step, step - 1, step + 1
+            if step + 2 < N_CHUNKS:
+                load_x2(step + 2)
+                load_x1(step + 2)
+            if now < N_CHUNKS:
+                tree_first_level(now)
+            if before >= 0:
+                transpose_r(before)
+            if ahead < N_CHUNKS:
+                transpose_x1(ahead)
+            if step == 0:
+                transpose_bias()
+            if before >= 0:
+                r_mx[before] = quantise(r_grouped[before], PAIRS, "r")
+            if now < N_CHUNKS:
+                x1_mx[now] = quantise(x1_grouped[now], CHUNK, "x1")
+            if step == 0:
+                nc.vector.quantize_mx(
+                    out=x0_codes[:].bitcast(FP8X4), scales=x0_scales[:], in_=x0_grouped[:].rearrange("p b t -> p (b t)")
+                )
+            if before >= 0:
+                multiply(before)
+            if now < N_CHUNKS:
+                tree_other_levels(now)

@@ -20,11 +20,9 @@ HALVES = SCENES // P
 PARTNERS = OBJECTS - 1
 RUN = OBJECTS * C2
 RUNS = OBJECTS - 1
-CHUNK = 4
-CHUNKS_PER_HALF = OBJECTS // CHUNK
-N_CHUNKS = HALVES * CHUNKS_PER_HALF
-PAIRS = CHUNK // 2
 OUT_HALVES = OUT // P
+CHUNK_SIZES = ((2, 2, 4, 4, 4), (4, 4, 4, 2, 2))
+N_CHUNKS = len(CHUNK_SIZES[0]) + len(CHUNK_SIZES[1])
 
 FLOPS = 2 * SCENES * OBJECTS * K * OUT
 BYTES = (
@@ -35,8 +33,17 @@ BYTES = (
 )
 
 
+def chunk_list():
+    chunks = []
+    for half, sizes in enumerate(CHUNK_SIZES):
+        for n, count in enumerate(sizes):
+            chunks.append((half, sum(sizes[:n]), count))
+    return chunks
+
+
 def tile_differentiablelogicmachine_pb_t_kernel(tc, x0, x1, x2, W1_words, W1_scales, b1, out):
     nc = tc.nc
+    CHUNKS = chunk_list()
     with ExitStack() as ctx:
         const = ctx.enter_context(tc.tile_pool(name="const", bufs=1))
         x2_pool = ctx.enter_context(tc.tile_pool(name="x2", bufs=HALVES))
@@ -54,27 +61,28 @@ def tile_differentiablelogicmachine_pb_t_kernel(tc, x0, x1, x2, W1_words, W1_sca
         x1_tiles = {}
 
         def load_x2(chunk):
-            half, part = divmod(chunk, CHUNKS_PER_HALF)
-            if part == 0:
+            half, first, count = CHUNKS[chunk]
+            if first == 0:
                 x2_sb = x2_pool.tile([P, RUNS, RUN], BF16)
                 x2_tiles[half] = x2_sb
             table = x2[half * P : (half + 1) * P].rearrange("b i j c -> b (i j c)")
             runs = table[:, C2:].rearrange("b (g r) -> b g r", r=RUN + C2)
-            g0, g1 = CHUNK * part, min(CHUNK * (part + 1), RUNS)
+            g0, g1 = first, min(first + count, RUNS)
             nc.sync.dma_start(out=x2_tiles[half][:, g0:g1, :], in_=runs[:, g0:g1, 0:RUN])
 
         def load_x1(chunk):
-            half, part = divmod(chunk, CHUNKS_PER_HALF)
-            x1_sb = x1_pool.tile([P, CHUNK, C1], BF16)
+            half, first, count = CHUNKS[chunk]
+            x1_sb = x1_pool.tile([P, count, C1], BF16)
             x1_tiles[chunk] = x1_sb
-            nc.sync.dma_start(
-                out=x1_sb[:], in_=x1[half * P : (half + 1) * P, CHUNK * part : CHUNK * (part + 1), :]
-            )
+            nc.sync.dma_start(out=x1_sb[:], in_=x1[half * P : (half + 1) * P, first : first + count, :])
 
         load_x2(0)
         load_x1(0)
         x0_sb = const.tile([P, HALVES, C0], BF16)
         nc.sync.dma_start(out=x0_sb[:], in_=x0.rearrange("(h b) k -> b h k", h=HALVES))
+        bias_rows = const.tile([P, P], BF16)
+        nc.vector.memset(bias_rows[:], 0.0)
+        nc.sync.dma_start(out=bias_rows[0:OUT_HALVES, :], in_=b1.rearrange("(h o) -> h o", h=OUT_HALVES))
         load_x2(1)
         load_x1(1)
 
@@ -86,8 +94,6 @@ def tile_differentiablelogicmachine_pb_t_kernel(tc, x0, x1, x2, W1_words, W1_sca
         s_high = const.tile([P, 2, OUT], U8, align_bytes=64)
         for zeroed in (w_low, w_high, s_x1, s_low, s_high):
             nc.vector.memset(zeroed[:].bitcast(I32), 0)
-        bias_rows = const.tile([P, P], BF16)
-        nc.vector.memset(bias_rows[:], 0.0)
         table_warmer = const.tile([P, 2], F32)
         nc.vector.memset(table_warmer[:, 0:1], 0.0)
         nc.scalar.activation(out=table_warmer[:, 1:2], in_=table_warmer[:, 0:1], func=ACT.Sigmoid)
@@ -103,7 +109,6 @@ def tile_differentiablelogicmachine_pb_t_kernel(tc, x0, x1, x2, W1_words, W1_sca
         )
         nc.sync.dma_start(out=w_low[0:64].bitcast(I32), in_=words_by_64[:, 0:4:3, :].bitcast(I32))
         nc.sync.dma_start(out=w_high[64:128].bitcast(I32), in_=words_by_64[:, 0:4:3, :].bitcast(I32))
-        nc.sync.dma_start(out=bias_rows[0:OUT_HALVES, :], in_=b1.rearrange("(h o) -> h o", h=OUT_HALVES))
         scales_by_8 = W1_scales.rearrange("g (s q) n -> q (g s) n", q=8)
         scale_rows = W1_scales.rearrange("g q n -> (g q) n")
         for quad in range(4):
@@ -141,23 +146,26 @@ def tile_differentiablelogicmachine_pb_t_kernel(tc, x0, x1, x2, W1_words, W1_sca
         r_grouped = {}
         x1_mx = {}
         r_mx = {}
+        sigmoids = {}
 
         def partners_of(chunk):
-            half, part = divmod(chunk, CHUNKS_PER_HALF)
+            half, first, count = CHUNKS[chunk]
             rows = x2_tiles[half][:].rearrange("b g r -> b (g r)").rearrange("b (i s c) -> b i s c", s=PARTNERS, c=C2)
-            return rows[:, CHUNK * part : CHUNK * (part + 1)]
+            return rows[:, first : first + count]
 
         def tree_first_level(chunk):
+            count = CHUNKS[chunk][2]
             x = partners_of(chunk)
-            top = tree_pool.tile([P, CHUNK, 7, C2], BF16)
-            low = tree_pool.tile([P, CHUNK, 7, C2], BF16)
+            top = tree_pool.tile([P, count, 7, C2], BF16)
+            low = tree_pool.tile([P, count, 7, C2], BF16)
             trees[chunk] = ((ALU.max, top), (ALU.min, low))
             for op, t in trees[chunk]:
                 nc.vector.tensor_tensor(out=t[:, :, 0:7, :], in0=x[:, :, 0:7, :], in1=x[:, :, 7:14, :], op=op)
 
         def tree_other_levels(chunk):
+            count = CHUNKS[chunk][2]
             x = partners_of(chunk)
-            r = tree_pool.tile([P, CHUNK, 2, C2], BF16)
+            r = tree_pool.tile([P, count, 2, C2], BF16)
             r_tiles[chunk] = r
             for op, t in trees[chunk]:
                 nc.vector.tensor_tensor(out=t[:, :, 3:6, :], in0=t[:, :, 0:3, :], in1=t[:, :, 3:6, :], op=op)
@@ -171,10 +179,11 @@ def tile_differentiablelogicmachine_pb_t_kernel(tc, x0, x1, x2, W1_words, W1_sca
             nc.vector.tensor_scalar_min(out=r[:, :, 1, :], in0=r[:, :, 1, :], scalar1=1.0)
 
         def transpose_x1(chunk):
+            count = CHUNKS[chunk][2]
             words = x1_tiles[chunk][:].rearrange("b a k -> b (a k)").bitcast(F32)
-            grouped = grouped_pool.tile([P, CHUNK, P, 4], BF16, align_bytes=64, tag="x1_grouped")
+            grouped = grouped_pool.tile([P, count, P, 4], BF16, align_bytes=64, tag="x1_grouped")
             x1_grouped[chunk] = grouped
-            for pair in range(PAIRS):
+            for pair in range(count // 2):
                 bank = psum_in.tile([P, 2, 2, P], F32, tag="bank_in")
                 for j in range(2):
                     transpose_words(bank[:, j], words, (2 * pair + j) * (C1 // 2))
@@ -183,15 +192,17 @@ def tile_differentiablelogicmachine_pb_t_kernel(tc, x0, x1, x2, W1_words, W1_sca
                 )
 
         def transpose_r(chunk):
+            pairs = CHUNKS[chunk][2] // 2
             words = r_tiles[chunk][:].rearrange("b a m c -> b (a m c)").bitcast(F32)
-            grouped = grouped_pool.tile([P, PAIRS, P, 4], BF16, align_bytes=64, tag="r_grouped")
+            grouped = grouped_pool.tile([P, pairs, P, 4], BF16, align_bytes=64, tag="r_grouped")
             r_grouped[chunk] = grouped
-            bank = psum_in.tile([P, PAIRS, 2, P], F32, tag="bank_in")
-            for pair in range(PAIRS):
+            bank = psum_in.tile([P, pairs, 2, P], F32, tag="bank_in")
+            for pair in range(pairs):
                 transpose_words(bank[:, pair], words, pair * 2 * C2)
             nc.scalar.copy(out=grouped[:].bitcast(F32), in_=bank[:].rearrange("p a u b -> p a b u"))
 
-        def quantise(grouped, columns, tag):
+        def quantise(grouped, tag):
+            columns = grouped.shape[1]
             codes = code_pool.tile([P, columns, P], U32, align_bytes=64, tag=tag + "_codes")
             scales = code_pool.tile([P, columns, P], U8, align_bytes=64, tag=tag + "_scales")
             nc.vector.quantize_mx(
@@ -202,17 +213,16 @@ def tile_differentiablelogicmachine_pb_t_kernel(tc, x0, x1, x2, W1_words, W1_sca
             return codes, scales
 
         def multiply(chunk):
-            half, part = divmod(chunk, CHUNKS_PER_HALF)
+            half, first, count = CHUNKS[chunk]
             x1_codes, x1_scales = x1_mx[chunk]
             r_codes, r_scales = r_mx[chunk]
             w_x0, s_x0 = (w_low, s_low) if half == 0 else (w_high, s_high)
-            result = out_pool.tile([P, CHUNK, OUT], F32, tag="result")
-            sigmoids = []
+            sigmoids[chunk] = []
             for oh in range(OUT_HALVES):
                 w_cols = slice(2 * P * oh, 2 * P * (oh + 1))
                 s_cols = slice(P * oh, P * (oh + 1))
-                acc = psum_acc.tile([P, CHUNK, P], F32, tag="acc")
-                for a in range(CHUNK):
+                acc = psum_acc.tile([P, count, P], F32, tag="acc")
+                for a in range(count):
                     pair, second = divmod(a, 2)
                     w_r, s_r = (w_low, s_low) if second == 0 else (w_high, s_high)
                     nc.tensor.matmul_mx(
@@ -242,42 +252,42 @@ def tile_differentiablelogicmachine_pb_t_kernel(tc, x0, x1, x2, W1_words, W1_sca
                         start=False,
                         stop=True,
                     )
-                sig = out_pool.tile([P, CHUNK, P], F32, tag="sig")
+                sig = out_pool.tile([P, count, P], F32, tag="sig")
                 nc.scalar.activation(out=sig[:], in_=acc[:], func=ACT.Sigmoid, bias=bias[:, oh : oh + 1], scale=1.0)
-                sigmoids.append(sig)
-            for oh in range(OUT_HALVES):
-                back = psum_out.tile([P, CHUNK, P], F32, tag="back")
-                for a in range(CHUNK):
-                    nc.tensor.transpose(back[:, a, :], sigmoids[oh][:, a, :], ident_f32[:])
-                nc.scalar.copy(out=result[:, :, P * oh : P * (oh + 1)], in_=back[:])
-            nc.sync.dma_start(
-                out=out[half * P : (half + 1) * P, CHUNK * part : CHUNK * (part + 1), :], in_=result[:]
-            )
+                sigmoids[chunk].append(sig)
 
-        transpose_x1(0)
-        transpose_x0()
-        for step in range(N_CHUNKS + 1):
-            now, before, ahead = step, step - 1, step + 1
+        def transpose_back_and_store(chunk):
+            half, first, count = CHUNKS[chunk]
+            result = out_pool.tile([P, count, OUT], F32, tag="result")
+            for oh in range(OUT_HALVES):
+                back = psum_out.tile([P, count, P], F32, tag="back")
+                for a in range(count):
+                    nc.tensor.transpose(back[:, a, :], sigmoids[chunk][oh][:, a, :], ident_f32[:])
+                nc.scalar.copy(out=result[:, :, P * oh : P * (oh + 1)], in_=back[:])
+            nc.sync.dma_start(out=out[half * P : (half + 1) * P, first : first + count, :], in_=result[:])
+
+        for step in range(N_CHUNKS + 2):
             if step + 2 < N_CHUNKS:
                 load_x2(step + 2)
                 load_x1(step + 2)
-            if now < N_CHUNKS:
-                tree_first_level(now)
-            if before >= 0:
-                transpose_r(before)
-            if ahead < N_CHUNKS:
-                transpose_x1(ahead)
+            if step < N_CHUNKS:
+                tree_first_level(step)
+            if 0 <= step - 1 < N_CHUNKS:
+                transpose_r(step - 1)
+            if 0 <= step - 2:
+                transpose_back_and_store(step - 2)
+            if step < N_CHUNKS:
+                transpose_x1(step)
             if step == 0:
+                transpose_x0()
                 transpose_bias()
-            if before >= 0:
-                r_mx[before] = quantise(r_grouped[before], PAIRS, "r")
-            if now < N_CHUNKS:
-                x1_mx[now] = quantise(x1_grouped[now], CHUNK, "x1")
-            if step == 0:
+            if step == 1:
                 nc.vector.quantize_mx(
                     out=x0_codes[:].bitcast(FP8X4), scales=x0_scales[:], in_=x0_grouped[:].rearrange("p b t -> p (b t)")
                 )
-            if before >= 0:
-                multiply(before)
-            if now < N_CHUNKS:
-                tree_other_levels(now)
+            if 0 <= step - 1 < N_CHUNKS:
+                x1_mx[step - 1] = quantise(x1_grouped[step - 1], "x1")
+                r_mx[step - 1] = quantise(r_grouped[step - 1], "r")
+                multiply(step - 1)
+            if step < N_CHUNKS:
+                tree_other_levels(step)

@@ -60,6 +60,10 @@ def tile_differentiablelogicmachine_pb_t_kernel(tc, x0, x1, x2, W1_words, W1_sca
         x2_tiles = {}
         x1_tiles = {}
 
+        def pieces_of(chunk):
+            count = CHUNKS[chunk][2]
+            return [(a, 1) for a in range(count)] if chunk == 0 else [(0, count)]
+
         def load_x2(chunk):
             half, first, count = CHUNKS[chunk]
             if first == 0:
@@ -67,8 +71,9 @@ def tile_differentiablelogicmachine_pb_t_kernel(tc, x0, x1, x2, W1_words, W1_sca
                 x2_tiles[half] = x2_sb
             table = x2[half * P : (half + 1) * P].rearrange("b i j c -> b (i j c)")
             runs = table[:, C2:].rearrange("b (g r) -> b g r", r=RUN + C2)
-            g0, g1 = first, min(first + count, RUNS)
-            nc.sync.dma_start(out=x2_tiles[half][:, g0:g1, :], in_=runs[:, g0:g1, 0:RUN])
+            for start, n in pieces_of(chunk):
+                g0, g1 = first + start, min(first + start + n, RUNS)
+                nc.sync.dma_start(out=x2_tiles[half][:, g0:g1, :], in_=runs[:, g0:g1, 0:RUN])
 
         def load_x1(chunk):
             half, first, count = CHUNKS[chunk]
@@ -141,6 +146,7 @@ def tile_differentiablelogicmachine_pb_t_kernel(tc, x0, x1, x2, W1_words, W1_sca
             nc.scalar.copy(out=bias[:], in_=bank[:, 0:OUT_HALVES])
 
         trees = {}
+        filled_14 = {}
         r_tiles = {}
         x1_grouped = {}
         r_grouped = {}
@@ -153,30 +159,37 @@ def tile_differentiablelogicmachine_pb_t_kernel(tc, x0, x1, x2, W1_words, W1_sca
             rows = x2_tiles[half][:].rearrange("b g r -> b (g r)").rearrange("b (i s c) -> b i s c", s=PARTNERS, c=C2)
             return rows[:, first : first + count]
 
+        def fill_of_maximum(chunk):
+            count = CHUNKS[chunk][2]
+            filled = tree_pool.tile([P, count, 2, C2], BF16)
+            filled_14[chunk] = filled
+            nc.scalar.activation(out=filled[:, :, 0, :], in_=partners_of(chunk)[:, :, 14, :], func=ACT.Relu)
+
         def tree_first_level(chunk):
             count = CHUNKS[chunk][2]
             x = partners_of(chunk)
             top = tree_pool.tile([P, count, 7, C2], BF16)
             low = tree_pool.tile([P, count, 7, C2], BF16)
             trees[chunk] = ((ALU.max, top), (ALU.min, low))
-            for op, t in trees[chunk]:
-                nc.vector.tensor_tensor(out=t[:, :, 0:7, :], in0=x[:, :, 0:7, :], in1=x[:, :, 7:14, :], op=op)
+            for start, n in pieces_of(chunk):
+                piece = slice(start, start + n)
+                for op, t in trees[chunk]:
+                    nc.vector.tensor_tensor(out=t[:, piece], in0=x[:, piece, 0:7, :], in1=x[:, piece, 7:14, :], op=op)
+            nc.vector.tensor_scalar_min(out=filled_14[chunk][:, :, 1, :], in0=x[:, :, 14, :], scalar1=1.0)
 
         def tree_other_levels(chunk):
             count = CHUNKS[chunk][2]
-            x = partners_of(chunk)
+            filled = filled_14[chunk]
             r = tree_pool.tile([P, count, 2, C2], BF16)
             r_tiles[chunk] = r
             for op, t in trees[chunk]:
                 nc.vector.tensor_tensor(out=t[:, :, 3:6, :], in0=t[:, :, 0:3, :], in1=t[:, :, 3:6, :], op=op)
-            for op, t in trees[chunk]:
-                nc.vector.tensor_tensor(out=t[:, :, 6, :], in0=t[:, :, 6, :], in1=x[:, :, 14, :], op=op)
+            for which, (op, t) in enumerate(trees[chunk]):
+                nc.vector.tensor_tensor(out=t[:, :, 6, :], in0=t[:, :, 6, :], in1=filled[:, :, which, :], op=op)
             for op, t in trees[chunk]:
                 nc.vector.tensor_tensor(out=t[:, :, 3:5, :], in0=t[:, :, 3:5, :], in1=t[:, :, 5:7, :], op=op)
             for which, (op, t) in enumerate(trees[chunk]):
                 nc.vector.tensor_tensor(out=r[:, :, which, :], in0=t[:, :, 3, :], in1=t[:, :, 4, :], op=op)
-            nc.vector.tensor_scalar_max(out=r[:, :, 0, :], in0=r[:, :, 0, :], scalar1=0.0)
-            nc.vector.tensor_scalar_min(out=r[:, :, 1, :], in0=r[:, :, 1, :], scalar1=1.0)
 
         def transpose_x1(chunk):
             count = CHUNKS[chunk][2]
@@ -266,6 +279,7 @@ def tile_differentiablelogicmachine_pb_t_kernel(tc, x0, x1, x2, W1_words, W1_sca
                 nc.scalar.copy(out=result[:, :, P * oh : P * (oh + 1)], in_=back[:])
             nc.sync.dma_start(out=out[half * P : (half + 1) * P, first : first + count, :], in_=result[:])
 
+        fill_of_maximum(0)
         for step in range(N_CHUNKS + 2):
             if step + 2 < N_CHUNKS:
                 load_x2(step + 2)
@@ -289,5 +303,7 @@ def tile_differentiablelogicmachine_pb_t_kernel(tc, x0, x1, x2, W1_words, W1_sca
                 x1_mx[step - 1] = quantise(x1_grouped[step - 1], "x1")
                 r_mx[step - 1] = quantise(r_grouped[step - 1], "r")
                 multiply(step - 1)
+            if step + 1 < N_CHUNKS:
+                fill_of_maximum(step + 1)
             if step < N_CHUNKS:
                 tree_other_levels(step)

@@ -23,6 +23,7 @@ RUNS = OBJECTS - 1
 OUT_HALVES = OUT // P
 CHUNK_SIZES = ((2, 2, 4, 4, 4), (4, 4, 4, 2, 2))
 N_CHUNKS = len(CHUNK_SIZES[0]) + len(CHUNK_SIZES[1])
+CATCHING_UP = 3
 
 FLOPS = 2 * SCENES * OBJECTS * K * OUT
 BYTES = (
@@ -62,7 +63,8 @@ def tile_differentiablelogicmachine_pb_t_kernel(tc, x0, x1, x2, W1_words, W1_sca
 
         def pieces_of(chunk):
             count = CHUNKS[chunk][2]
-            return [(a, 1) for a in range(count)] if chunk == 0 else [(0, count)]
+            size = 1 if chunk == 0 else 2 if chunk < CATCHING_UP else count
+            return [(start, size) for start in range(0, count, size)]
 
         def load_x2(chunk):
             half, first, count = CHUNKS[chunk]
@@ -89,6 +91,7 @@ def tile_differentiablelogicmachine_pb_t_kernel(tc, x0, x1, x2, W1_words, W1_sca
         nc.vector.memset(bias_rows[:], 0.0)
         nc.sync.dma_start(out=bias_rows[0:OUT_HALVES, :], in_=b1.rearrange("(h o) -> h o", h=OUT_HALVES))
         load_x2(1)
+        load_x2(2)
         load_x1(1)
 
         w_x1 = const.tile([P, 2 * OUT], U8, align_bytes=64)
@@ -146,7 +149,6 @@ def tile_differentiablelogicmachine_pb_t_kernel(tc, x0, x1, x2, W1_words, W1_sca
             nc.scalar.copy(out=bias[:], in_=bank[:, 0:OUT_HALVES])
 
         trees = {}
-        filled_14 = {}
         r_tiles = {}
         x1_grouped = {}
         r_grouped = {}
@@ -159,37 +161,35 @@ def tile_differentiablelogicmachine_pb_t_kernel(tc, x0, x1, x2, W1_words, W1_sca
             rows = x2_tiles[half][:].rearrange("b g r -> b (g r)").rearrange("b (i s c) -> b i s c", s=PARTNERS, c=C2)
             return rows[:, first : first + count]
 
-        def fill_of_maximum(chunk):
+        def start_trees(chunk):
             count = CHUNKS[chunk][2]
-            filled = tree_pool.tile([P, count, 2, C2], BF16)
-            filled_14[chunk] = filled
-            nc.scalar.activation(out=filled[:, :, 0, :], in_=partners_of(chunk)[:, :, 14, :], func=ACT.Relu)
+            top = tree_pool.tile([P, count, 8, C2], BF16)
+            low = tree_pool.tile([P, count, 8, C2], BF16)
+            trees[chunk] = ((ALU.max, top), (ALU.min, low))
+            nc.scalar.activation(out=top[:, :, 7, :], in_=partners_of(chunk)[:, :, 14, :], func=ACT.Relu)
 
         def tree_first_level(chunk):
-            count = CHUNKS[chunk][2]
             x = partners_of(chunk)
-            top = tree_pool.tile([P, count, 7, C2], BF16)
-            low = tree_pool.tile([P, count, 7, C2], BF16)
-            trees[chunk] = ((ALU.max, top), (ALU.min, low))
             for start, n in pieces_of(chunk):
                 piece = slice(start, start + n)
                 for op, t in trees[chunk]:
-                    nc.vector.tensor_tensor(out=t[:, piece], in0=x[:, piece, 0:7, :], in1=x[:, piece, 7:14, :], op=op)
-            nc.vector.tensor_scalar_min(out=filled_14[chunk][:, :, 1, :], in0=x[:, :, 14, :], scalar1=1.0)
+                    nc.vector.tensor_tensor(
+                        out=t[:, piece, 0:7, :], in0=x[:, piece, 0:7, :], in1=x[:, piece, 7:14, :], op=op
+                    )
+            low = trees[chunk][1][1]
+            nc.vector.tensor_scalar_min(out=low[:, :, 7, :], in0=x[:, :, 14, :], scalar1=1.0)
 
         def tree_other_levels(chunk):
             count = CHUNKS[chunk][2]
-            filled = filled_14[chunk]
             r = tree_pool.tile([P, count, 2, C2], BF16)
             r_tiles[chunk] = r
-            for op, t in trees[chunk]:
-                nc.vector.tensor_tensor(out=t[:, :, 3:6, :], in0=t[:, :, 0:3, :], in1=t[:, :, 3:6, :], op=op)
+            for width in (4, 2):
+                for op, t in trees[chunk]:
+                    nc.vector.tensor_tensor(
+                        out=t[:, :, 0:width, :], in0=t[:, :, 0:width, :], in1=t[:, :, width : 2 * width, :], op=op
+                    )
             for which, (op, t) in enumerate(trees[chunk]):
-                nc.vector.tensor_tensor(out=t[:, :, 6, :], in0=t[:, :, 6, :], in1=filled[:, :, which, :], op=op)
-            for op, t in trees[chunk]:
-                nc.vector.tensor_tensor(out=t[:, :, 3:5, :], in0=t[:, :, 3:5, :], in1=t[:, :, 5:7, :], op=op)
-            for which, (op, t) in enumerate(trees[chunk]):
-                nc.vector.tensor_tensor(out=r[:, :, which, :], in0=t[:, :, 3, :], in1=t[:, :, 4, :], op=op)
+                nc.vector.tensor_tensor(out=r[:, :, which, :], in0=t[:, :, 0, :], in1=t[:, :, 1, :], op=op)
 
         def transpose_x1(chunk):
             count = CHUNKS[chunk][2]
@@ -279,10 +279,11 @@ def tile_differentiablelogicmachine_pb_t_kernel(tc, x0, x1, x2, W1_words, W1_sca
                 nc.scalar.copy(out=result[:, :, P * oh : P * (oh + 1)], in_=back[:])
             nc.sync.dma_start(out=out[half * P : (half + 1) * P, first : first + count, :], in_=result[:])
 
-        fill_of_maximum(0)
+        start_trees(0)
         for step in range(N_CHUNKS + 2):
+            if step + 3 < N_CHUNKS:
+                load_x2(step + 3)
             if step + 2 < N_CHUNKS:
-                load_x2(step + 2)
                 load_x1(step + 2)
             if step < N_CHUNKS:
                 tree_first_level(step)
@@ -304,6 +305,6 @@ def tile_differentiablelogicmachine_pb_t_kernel(tc, x0, x1, x2, W1_words, W1_sca
                 r_mx[step - 1] = quantise(r_grouped[step - 1], "r")
                 multiply(step - 1)
             if step + 1 < N_CHUNKS:
-                fill_of_maximum(step + 1)
+                start_trees(step + 1)
             if step < N_CHUNKS:
                 tree_other_levels(step)

@@ -188,6 +188,8 @@ def tile_differentiablelogicmachine_pb_t_kernel(tc, x0, x1, x2, W1_words, W1_sca
                     nc.vector.tensor_tensor(
                         out=t[:, :, 0:width, :], in0=t[:, :, 0:width, :], in1=t[:, :, width : 2 * width, :], op=op
                     )
+            if chunk > 0:
+                quantise_chunk(chunk - 1)
             for which, (op, t) in enumerate(trees[chunk]):
                 nc.vector.tensor_tensor(out=r[:, :, which, :], in0=t[:, :, 0, :], in1=t[:, :, 1, :], op=op)
 
@@ -224,6 +226,10 @@ def tile_differentiablelogicmachine_pb_t_kernel(tc, x0, x1, x2, W1_words, W1_sca
                 in_=grouped[:].rearrange("p a b t -> p (a b t)"),
             )
             return codes, scales
+
+        def quantise_chunk(chunk):
+            x1_mx[chunk] = quantise(x1_grouped[chunk], "x1")
+            r_mx[chunk] = quantise(r_grouped[chunk], "r")
 
         def multiply(chunk):
             half, first, count = CHUNKS[chunk]
@@ -300,11 +306,11 @@ def tile_differentiablelogicmachine_pb_t_kernel(tc, x0, x1, x2, W1_words, W1_sca
                 nc.vector.quantize_mx(
                     out=x0_codes[:].bitcast(FP8X4), scales=x0_scales[:], in_=x0_grouped[:].rearrange("p b t -> p (b t)")
                 )
-            if 0 <= step - 1 < N_CHUNKS:
-                x1_mx[step - 1] = quantise(x1_grouped[step - 1], "x1")
-                r_mx[step - 1] = quantise(r_grouped[step - 1], "r")
-                multiply(step - 1)
             if step + 1 < N_CHUNKS:
                 start_trees(step + 1)
             if step < N_CHUNKS:
                 tree_other_levels(step)
+            elif step == N_CHUNKS:
+                quantise_chunk(step - 1)
+            if 0 <= step - 1 < N_CHUNKS:
+                multiply(step - 1)

@@ -22,6 +22,8 @@ RUN = OBJECTS * C2
 RUNS = OBJECTS - 1
 OUT_HALVES = OUT // P
 CHUNK_SIZES = ((2, 2, 4, 4, 4), (4, 4, 4, 2, 2))
+X0_LOW, X0_TWIN, X0_HIGH, X1, R_LOW, R_HIGH, N_SECTIONS = 0, 1, 2, 4, 6, 7, 8
+S_X0_TWIN, S_X0, S_X1, S_R, S_R_TWIN, N_SCALE_SECTIONS = 0, 1, 2, 4, 5, 6
 N_CHUNKS = len(CHUNK_SIZES[0]) + len(CHUNK_SIZES[1])
 CATCHING_UP = 3
 
@@ -45,16 +47,18 @@ def chunk_list():
 def tile_differentiablelogicmachine_pb_t_kernel(tc, x0, x1, x2, W1_words, W1_scales, b1, out):
     nc = tc.nc
     CHUNKS = chunk_list()
+    last = N_CHUNKS - 1
     with ExitStack() as ctx:
         const = ctx.enter_context(tc.tile_pool(name="const", bufs=1))
         x2_pool = ctx.enter_context(tc.tile_pool(name="x2", bufs=HALVES))
         x1_pool = ctx.enter_context(tc.tile_pool(name="x1", bufs=3))
         tree_pool = ctx.enter_context(tc.tile_pool(name="tree", bufs=2))
-        grouped_pool = ctx.enter_context(tc.tile_pool(name="grouped", bufs=2))
-        code_pool = ctx.enter_context(tc.tile_pool(name="codes", bufs=2))
+        grouped_pool = ctx.enter_context(tc.tile_pool(name="grouped", bufs=3))
+        code_pool = ctx.enter_context(tc.tile_pool(name="codes", bufs=3))
         out_pool = ctx.enter_context(tc.tile_pool(name="outs", bufs=2))
+        pair_pool = ctx.enter_context(tc.tile_pool(name="pair_outs", bufs=4))
         psum_in = ctx.enter_context(tc.psum_pool(name="psum_in", bufs=3))
-        psum_acc = ctx.enter_context(tc.psum_pool(name="psum_acc", bufs=2))
+        psum_acc = ctx.enter_context(tc.psum_pool(name="psum_acc", bufs=3))
         psum_out = ctx.enter_context(tc.psum_pool(name="psum_out", bufs=2))
         ctx.enter_context(tc.manual_schedule())
 
@@ -83,25 +87,21 @@ def tile_differentiablelogicmachine_pb_t_kernel(tc, x0, x1, x2, W1_words, W1_sca
             x1_tiles[chunk] = x1_sb
             nc.sync.dma_start(out=x1_sb[:], in_=x1[half * P : (half + 1) * P, first : first + count, :])
 
-        load_x2(0)
-        load_x1(0)
         x0_sb = const.tile([P, HALVES, C0], BF16)
-        nc.sync.dma_start(out=x0_sb[:], in_=x0.rearrange("(h b) k -> b h k", h=HALVES))
         bias_rows = const.tile([P, P], BF16)
         nc.vector.memset(bias_rows[:], 0.0)
-        nc.sync.dma_start(out=bias_rows[0:OUT_HALVES, :], in_=b1.rearrange("(h o) -> h o", h=OUT_HALVES))
+        load_x2(0)
         load_x2(1)
+        load_x1(0)
+        nc.sync.dma_start(out=x0_sb[:], in_=x0.rearrange("(h b) k -> b h k", h=HALVES))
         load_x2(2)
         load_x1(1)
 
-        w_x1 = const.tile([P, 2 * OUT], U8, align_bytes=64)
-        w_low = const.tile([P, 2, 2 * OUT], U8, align_bytes=64)
-        w_high = const.tile([P, 2, 2 * OUT], U8, align_bytes=64)
-        s_x1 = const.tile([P, OUT], U8, align_bytes=64)
-        s_low = const.tile([P, 2, OUT], U8, align_bytes=64)
-        s_high = const.tile([P, 2, OUT], U8, align_bytes=64)
-        for zeroed in (w_low, w_high, s_x1, s_low, s_high):
-            nc.vector.memset(zeroed[:].bitcast(I32), 0)
+        weights = const.tile([P, N_SECTIONS, 2 * OUT], U8, align_bytes=64)
+        weight_scales = const.tile([P, N_SCALE_SECTIONS, OUT], U8, align_bytes=64)
+        nc.vector.memset(weights[:, 0:X1].bitcast(I32), 0)
+        nc.vector.memset(weights[:, X1 + 1 :].bitcast(I32), 0)
+        nc.vector.memset(weight_scales[:].bitcast(I32), 0)
         table_warmer = const.tile([P, 2], F32)
         nc.vector.memset(table_warmer[:, 0:1], 0.0)
         nc.scalar.activation(out=table_warmer[:, 1:2], in_=table_warmer[:, 0:1], func=ACT.Sigmoid)
@@ -112,22 +112,38 @@ def tile_differentiablelogicmachine_pb_t_kernel(tc, x0, x1, x2, W1_words, W1_sca
         make_identity(nc, ident_bf16[:])
 
         words_by_64 = W1_words.rearrange("g (s p) n -> p (g s) n", p=64)
-        nc.sync.dma_start(
-            out=w_x1[:].bitcast(I32), in_=W1_words.rearrange("g p n -> (g p) n")[64:192, :].bitcast(I32)
-        )
-        nc.sync.dma_start(out=w_low[0:64].bitcast(I32), in_=words_by_64[:, 0:4:3, :].bitcast(I32))
-        nc.sync.dma_start(out=w_high[64:128].bitcast(I32), in_=words_by_64[:, 0:4:3, :].bitcast(I32))
+        x0_and_r = words_by_64[:, 0:4:3, :].bitcast(I32)
         scales_by_8 = W1_scales.rearrange("g (s q) n -> q (g s) n", q=8)
-        scale_rows = W1_scales.rearrange("g q n -> (g q) n")
-        for quad in range(4):
+
+        bias_row = const.tile([P, OUT], BF16)
+
+        def load_weight():
             nc.sync.dma_start(
-                out=s_x1[32 * quad : 32 * quad + 4, :].bitcast(I32),
-                in_=scale_rows[8 + 4 * quad : 12 + 4 * quad, :].bitcast(I32),
+                out=weights[:, X1].bitcast(I32), in_=W1_words.rearrange("g p n -> (g p) n")[64:192, :].bitcast(I32)
             )
-        for quad in range(2):
-            rows = scales_by_8[4 * quad : 4 * quad + 4, 0:4:3, :].bitcast(I32)
-            nc.sync.dma_start(out=s_low[32 * quad : 32 * quad + 4].bitcast(I32), in_=rows)
-            nc.sync.dma_start(out=s_high[64 + 32 * quad : 64 + 32 * quad + 4].bitcast(I32), in_=rows)
+            nc.sync.dma_start(out=weights[0:64, X0_LOW : R_LOW + 1 : R_LOW - X0_LOW].bitcast(I32), in_=x0_and_r)
+            nc.sync.dma_start(out=weights[64:128, X0_HIGH : R_HIGH + 1 : R_HIGH - X0_HIGH].bitcast(I32), in_=x0_and_r)
+            for quad in range(4):
+                rows = scales_by_8[4 * (quad % 2) : 4 * (quad % 2) + 4].bitcast(I32)
+                plane = weight_scales[32 * quad : 32 * quad + 4]
+                if quad < 2:
+                    nc.sync.dma_start(out=plane[:, S_X0 : S_R + 1].bitcast(I32), in_=rows)
+                else:
+                    nc.sync.dma_start(out=plane[:, S_X0 : S_R + 1 : S_R - S_X0].bitcast(I32), in_=rows[:, 0:4:3])
+                    nc.sync.dma_start(out=plane[:, S_X1].bitcast(I32), in_=rows[:, 2])
+
+        def load_twins():
+            nc.sync.dma_start(out=weights[64:128, X0_TWIN].bitcast(I32), in_=words_by_64[:, 0, :].bitcast(I32))
+            for quad in range(2, 4):
+                rows = scales_by_8[4 * (quad % 2) : 4 * (quad % 2) + 4].bitcast(I32)
+                plane = weight_scales[32 * quad : 32 * quad + 4]
+                nc.sync.dma_start(
+                    out=plane[:, S_X0_TWIN : S_R_TWIN + 1 : S_R_TWIN - S_X0_TWIN].bitcast(I32), in_=rows[:, 0:4:3]
+                )
+            nc.sync.dma_start(out=bias_row[:], in_=b1.partition_broadcast(P))
+
+        nc.sync.dma_start(out=bias_rows[0:OUT_HALVES, :], in_=b1.rearrange("(h o) -> h o", h=OUT_HALVES))
+        load_weight()
 
         def transpose_words(bank_part, words, first):
             for u in range(2):
@@ -179,7 +195,7 @@ def tile_differentiablelogicmachine_pb_t_kernel(tc, x0, x1, x2, W1_words, W1_sca
             low = trees[chunk][1][1]
             nc.vector.tensor_scalar_min(out=low[:, :, 7, :], in0=x[:, :, 14, :], scalar1=1.0)
 
-        def tree_other_levels(chunk):
+        def tree_other_levels(chunk, quantise_before_last_level):
             count = CHUNKS[chunk][2]
             r = tree_pool.tile([P, count, 2, C2], BF16)
             r_tiles[chunk] = r
@@ -188,8 +204,7 @@ def tile_differentiablelogicmachine_pb_t_kernel(tc, x0, x1, x2, W1_words, W1_sca
                     nc.vector.tensor_tensor(
                         out=t[:, :, 0:width, :], in0=t[:, :, 0:width, :], in1=t[:, :, width : 2 * width, :], op=op
                     )
-            if chunk > 0:
-                quantise_chunk(chunk - 1)
+            quantise_before_last_level()
             for which, (op, t) in enumerate(trees[chunk]):
                 nc.vector.tensor_tensor(out=r[:, :, which, :], in0=t[:, :, 0, :], in1=t[:, :, 1, :], op=op)
 
@@ -227,15 +242,25 @@ def tile_differentiablelogicmachine_pb_t_kernel(tc, x0, x1, x2, W1_words, W1_sca
             )
             return codes, scales
 
-        def quantise_chunk(chunk):
+        def quantise_x1(chunk):
             x1_mx[chunk] = quantise(x1_grouped[chunk], "x1")
+
+        def quantise_r(chunk):
             r_mx[chunk] = quantise(r_grouped[chunk], "r")
+
+        def quantise_for(step):
+            if 1 <= step < last:
+                quantise_x1(step - 1)
+            if step >= 1:
+                quantise_r(step - 1)
+            if step >= last - 1:
+                quantise_x1(step)
 
         def multiply(chunk):
             half, first, count = CHUNKS[chunk]
             x1_codes, x1_scales = x1_mx[chunk]
             r_codes, r_scales = r_mx[chunk]
-            w_x0, s_x0 = (w_low, s_low) if half == 0 else (w_high, s_high)
+            x0_section = X0_LOW if half == 0 else X0_HIGH
             sigmoids[chunk] = []
             for oh in range(OUT_HALVES):
                 w_cols = slice(2 * P * oh, 2 * P * (oh + 1))
@@ -243,11 +268,11 @@ def tile_differentiablelogicmachine_pb_t_kernel(tc, x0, x1, x2, W1_words, W1_sca
                 acc = psum_acc.tile([P, count, P], F32, tag="acc")
                 for a in range(count):
                     pair, second = divmod(a, 2)
-                    w_r, s_r = (w_low, s_low) if second == 0 else (w_high, s_high)
+                    r_section = R_LOW if second == 0 else R_HIGH
                     nc.tensor.matmul_mx(
                         out=acc[:, a, :],
-                        lhsT=w_x1[:, w_cols].bitcast(FP4X4),
-                        lhsT_scale=s_x1[:, s_cols],
+                        lhsT=weights[:, X1, w_cols].bitcast(FP4X4),
+                        lhsT_scale=weight_scales[:, S_X1, s_cols],
                         rhs=x1_codes[:, a, :].bitcast(FP8X4),
                         rhs_scale=x1_scales[:, a, :],
                         start=True,
@@ -255,8 +280,8 @@ def tile_differentiablelogicmachine_pb_t_kernel(tc, x0, x1, x2, W1_words, W1_sca
                     )
                     nc.tensor.matmul_mx(
                         out=acc[:, a, :],
-                        lhsT=w_x0[:, 0, w_cols].bitcast(FP4X4),
-                        lhsT_scale=s_x0[:, 0, s_cols],
+                        lhsT=weights[:, x0_section, w_cols].bitcast(FP4X4),
+                        lhsT_scale=weight_scales[:, S_X0, s_cols],
                         rhs=x0_codes[:].bitcast(FP8X4),
                         rhs_scale=x0_scales[:],
                         start=False,
@@ -264,8 +289,8 @@ def tile_differentiablelogicmachine_pb_t_kernel(tc, x0, x1, x2, W1_words, W1_sca
                     )
                     nc.tensor.matmul_mx(
                         out=acc[:, a, :],
-                        lhsT=w_r[:, 1, w_cols].bitcast(FP4X4),
-                        lhsT_scale=s_r[:, 1, s_cols],
+                        lhsT=weights[:, r_section, w_cols].bitcast(FP4X4),
+                        lhsT_scale=weight_scales[:, S_R, s_cols],
                         rhs=r_codes[:, pair, :].bitcast(FP8X4),
                         rhs_scale=r_scales[:, pair, :],
                         start=False,
@@ -274,6 +299,40 @@ def tile_differentiablelogicmachine_pb_t_kernel(tc, x0, x1, x2, W1_words, W1_sca
                 sig = out_pool.tile([P, count, P], F32, tag="sig")
                 nc.scalar.activation(out=sig[:], in_=acc[:], func=ACT.Sigmoid, bias=bias[:, oh : oh + 1], scale=1.0)
                 sigmoids[chunk].append(sig)
+
+        pair_accs = {}
+
+        def pair_pass(acc, codes, code_scales, section, scale_section, start, stop):
+            nc.tensor.matmul_mx(
+                out=acc[:].rearrange("p a n -> p (a n)"),
+                lhsT=codes.bitcast(FP8X4),
+                lhsT_scale=code_scales,
+                rhs=weights[:, section : section + 2, :].rearrange("p s n -> p (s n)").bitcast(FP4X4),
+                rhs_scale=weight_scales[:, scale_section : scale_section + 2, :].rearrange("p s n -> p (s n)"),
+                start=start,
+                stop=stop,
+            )
+
+        def start_pair(chunk):
+            acc = psum_acc.tile([P, 2, OUT], F32, tag="acc")
+            pair_accs[chunk] = acc
+            codes, code_scales = x1_mx[chunk]
+            pair_pass(acc, codes[:, 0, :], code_scales[:, 0, :], X1, S_X1, True, False)
+            pair_pass(acc, codes[:, 1, :], code_scales[:, 1, :], X1 - 1, S_X1 - 1, False, False)
+            pair_pass(acc, x0_codes[:], x0_scales[:], X0_TWIN, S_X0_TWIN, False, False)
+
+        def add_r(chunk):
+            codes, code_scales = r_mx[chunk]
+            pair_pass(pair_accs[chunk], codes[:, 0, :], code_scales[:, 0, :], R_LOW, S_R, False, True)
+
+        def finish_pair(chunk):
+            half, first, count = CHUNKS[chunk]
+            for a in range(count):
+                biased = pair_pool.tile([P, OUT], F32, tag="biased")
+                nc.vector.tensor_tensor(out=biased[:], in0=pair_accs[chunk][:, a, :], in1=bias_row[:], op=ALU.add)
+                last_out = pair_pool.tile([P, OUT], F32, tag="last_out")
+                nc.scalar.activation(out=last_out[:], in_=biased[:], func=ACT.Sigmoid)
+                nc.sync.dma_start(out=out[half * P : (half + 1) * P, first + a, :], in_=last_out[:])
 
         def transpose_back_and_store(chunk):
             half, first, count = CHUNKS[chunk]
@@ -286,31 +345,41 @@ def tile_differentiablelogicmachine_pb_t_kernel(tc, x0, x1, x2, W1_words, W1_sca
             nc.sync.dma_start(out=out[half * P : (half + 1) * P, first : first + count, :], in_=result[:])
 
         start_trees(0)
-        for step in range(N_CHUNKS + 2):
+        for step in range(N_CHUNKS):
             if step + 3 < N_CHUNKS:
                 load_x2(step + 3)
             if step + 2 < N_CHUNKS:
                 load_x1(step + 2)
-            if step < N_CHUNKS:
-                tree_first_level(step)
-            if 0 <= step - 1 < N_CHUNKS:
+            if step + 2 == last:
+                load_twins()
+            tree_first_level(step)
+            if step >= 1:
                 transpose_r(step - 1)
-            if 0 <= step - 2:
+            if step >= 2:
                 transpose_back_and_store(step - 2)
-            if step < N_CHUNKS:
+            if step < last - 1:
                 transpose_x1(step)
+            if last - 2 <= step < last:
+                transpose_x1(step + 1)
             if step == 0:
                 transpose_x0()
-                transpose_bias()
             if step == 1:
                 nc.vector.quantize_mx(
                     out=x0_codes[:].bitcast(FP8X4), scales=x0_scales[:], in_=x0_grouped[:].rearrange("p b t -> p (b t)")
                 )
-            if step + 1 < N_CHUNKS:
+            if step < last:
                 start_trees(step + 1)
-            if step < N_CHUNKS:
-                tree_other_levels(step)
-            elif step == N_CHUNKS:
-                quantise_chunk(step - 1)
-            if 0 <= step - 1 < N_CHUNKS:
+            tree_other_levels(step, lambda: quantise_for(step))
+            if step == 1:
+                transpose_bias()
+            if 1 <= step < last:
                 multiply(step - 1)
+            if step == last - 1:
+                start_pair(last - 1)
+        add_r(last - 1)
+        transpose_r(last)
+        start_pair(last)
+        finish_pair(last - 1)
+        quantise_r(last)
+        add_r(last)
+        finish_pair(last)

@@ -20,12 +20,14 @@ HALVES = SCENES // P
 PARTNERS = OBJECTS - 1
 RUN = OBJECTS * C2
 RUNS = OBJECTS - 1
+RUN_HALVES = ((0, RUN // 2), (RUN // 2, RUN))
 OUT_HALVES = OUT // P
 CHUNK_SIZES = ((2, 2, 4, 4, 4), (4, 4, 4, 2, 2))
 X0_LOW, X0_TWIN, X0_HIGH, X1, R_LOW, R_HIGH, N_SECTIONS = 0, 1, 2, 4, 6, 7, 8
 S_X0_TWIN, S_X0, S_X1, S_R, S_R_TWIN, N_SCALE_SECTIONS = 0, 1, 2, 4, 5, 6
+LATE = 2
 N_CHUNKS = len(CHUNK_SIZES[0]) + len(CHUNK_SIZES[1])
-CATCHING_UP = 3
+CATCHING_UP = 4
 
 FLOPS = 2 * SCENES * OBJECTS * K * OUT
 BYTES = (
@@ -79,7 +81,8 @@ def tile_differentiablelogicmachine_pb_t_kernel(tc, x0, x1, x2, W1_words, W1_sca
             runs = table[:, C2:].rearrange("b (g r) -> b g r", r=RUN + C2)
             for start, n in pieces_of(chunk):
                 g0, g1 = first + start, min(first + start + n, RUNS)
-                nc.sync.dma_start(out=x2_tiles[half][:, g0:g1, :], in_=runs[:, g0:g1, 0:RUN])
+                for r0, r1 in RUN_HALVES if chunk == 0 else ((0, RUN),):
+                    nc.sync.dma_start(out=x2_tiles[half][:, g0:g1, r0:r1], in_=runs[:, g0:g1, r0:r1])
 
         def load_x1(chunk):
             half, first, count = CHUNKS[chunk]
@@ -92,9 +95,9 @@ def tile_differentiablelogicmachine_pb_t_kernel(tc, x0, x1, x2, W1_words, W1_sca
         nc.vector.memset(bias_rows[:], 0.0)
         load_x2(0)
         load_x2(1)
+        load_x2(2)
         load_x1(0)
         nc.sync.dma_start(out=x0_sb[:], in_=x0.rearrange("(h b) k -> b h k", h=HALVES))
-        load_x2(2)
         load_x1(1)
 
         weights = const.tile([P, N_SECTIONS, 2 * OUT], U8, align_bytes=64)
@@ -188,10 +191,15 @@ def tile_differentiablelogicmachine_pb_t_kernel(tc, x0, x1, x2, W1_words, W1_sca
             x = partners_of(chunk)
             for start, n in pieces_of(chunk):
                 piece = slice(start, start + n)
-                for op, t in trees[chunk]:
-                    nc.vector.tensor_tensor(
-                        out=t[:, piece, 0:7, :], in0=x[:, piece, 0:7, :], in1=x[:, piece, 7:14, :], op=op
-                    )
+                for place, pairs in ((0, 4), (4, 3)) if chunk == 0 else ((0, 7),):
+                    one, other = 2 * place, 2 * place + pairs
+                    for op, t in trees[chunk]:
+                        nc.vector.tensor_tensor(
+                            out=t[:, piece, place : place + pairs, :],
+                            in0=x[:, piece, one : one + pairs, :],
+                            in1=x[:, piece, other : other + pairs, :],
+                            op=op,
+                        )
             low = trees[chunk][1][1]
             nc.vector.tensor_scalar_min(out=low[:, :, 7, :], in0=x[:, :, 14, :], scalar1=1.0)
 
@@ -249,9 +257,16 @@ def tile_differentiablelogicmachine_pb_t_kernel(tc, x0, x1, x2, W1_words, W1_sca
             r_mx[chunk] = quantise(r_grouped[chunk], "r")
 
         def quantise_for(step):
-            if 1 <= step < last:
+            if step == LATE:
+                nc.vector.quantize_mx(
+                    out=x0_codes[:].bitcast(FP8X4), scales=x0_scales[:], in_=x0_grouped[:].rearrange("p b t -> p (b t)")
+                )
+                for chunk in range(LATE - 1):
+                    quantise_x1(chunk)
+                    quantise_r(chunk)
+            if LATE <= step < last:
                 quantise_x1(step - 1)
-            if step >= 1:
+            if LATE <= step:
                 quantise_r(step - 1)
             if step >= last - 1:
                 quantise_x1(step)
@@ -355,24 +370,25 @@ def tile_differentiablelogicmachine_pb_t_kernel(tc, x0, x1, x2, W1_words, W1_sca
             tree_first_level(step)
             if step >= 1:
                 transpose_r(step - 1)
-            if step >= 2:
+            if step == LATE:
+                transpose_x0()
+                for chunk in range(LATE):
+                    transpose_x1(chunk)
+            if step > LATE:
                 transpose_back_and_store(step - 2)
-            if step < last - 1:
+            if LATE <= step < last - 1:
                 transpose_x1(step)
             if last - 2 <= step < last:
                 transpose_x1(step + 1)
-            if step == 0:
-                transpose_x0()
-            if step == 1:
-                nc.vector.quantize_mx(
-                    out=x0_codes[:].bitcast(FP8X4), scales=x0_scales[:], in_=x0_grouped[:].rearrange("p b t -> p (b t)")
-                )
             if step < last:
                 start_trees(step + 1)
             tree_other_levels(step, lambda: quantise_for(step))
-            if step == 1:
+            if step == LATE:
                 transpose_bias()
-            if 1 <= step < last:
+                for chunk in range(LATE - 1):
+                    multiply(chunk)
+                    transpose_back_and_store(chunk)
+            if LATE <= step < last:
                 multiply(step - 1)
             if step == last - 1:
                 start_pair(last - 1)

@@ -22,12 +22,12 @@ RUN = OBJECTS * C2
 RUNS = OBJECTS - 1
 RUN_HALVES = ((0, RUN // 2), (RUN // 2, RUN))
 OUT_HALVES = OUT // P
-CHUNK_SIZES = ((2, 2, 4, 4, 4), (4, 4, 4, 2, 2))
+TREE_SIZES = ((2, 2, 4, 8), (8, 4, 2, 2))
+BATCH = 4
+CATCHING_UP = 3
 X0_LOW, X0_TWIN, X0_HIGH, X1, R_LOW, R_HIGH, N_SECTIONS = 0, 1, 2, 4, 6, 7, 8
 S_X0_TWIN, S_X0, S_X1, S_R, S_R_TWIN, N_SCALE_SECTIONS = 0, 1, 2, 4, 5, 6
 LATE = 2
-N_CHUNKS = len(CHUNK_SIZES[0]) + len(CHUNK_SIZES[1])
-CATCHING_UP = 4
 
 FLOPS = 2 * SCENES * OBJECTS * K * OUT
 BYTES = (
@@ -38,27 +38,50 @@ BYTES = (
 )
 
 
-def chunk_list():
-    chunks = []
-    for half, sizes in enumerate(CHUNK_SIZES):
+def tree_list():
+    trees = []
+    for half, sizes in enumerate(TREE_SIZES):
         for n, count in enumerate(sizes):
-            chunks.append((half, sum(sizes[:n]), count))
-    return chunks
+            trees.append((half, sum(sizes[:n]), count))
+    return trees
+
+
+def batch_list(trees):
+    batches = []
+    for tree, (half, first, count) in enumerate(trees):
+        for start in range(0, count, BATCH):
+            batches.append((tree, start, min(BATCH, count - start)))
+    return batches
 
 
 def tile_differentiablelogicmachine_pb_t_kernel(tc, x0, x1, x2, W1_words, W1_scales, b1, out):
     nc = tc.nc
-    CHUNKS = chunk_list()
-    last = N_CHUNKS - 1
+    TREES = tree_list()
+    BATCHES = batch_list(TREES)
+    last_tree = len(TREES) - 1
+    last = len(BATCHES) - 1
+
+    def batches_of(tree):
+        return [batch for batch, (owner, start, count) in enumerate(BATCHES) if owner == tree]
+
+    def place_of(batch):
+        tree, start, count = BATCHES[batch]
+        return TREES[tree][0], TREES[tree][1] + start, count
+
     with ExitStack() as ctx:
         const = ctx.enter_context(tc.tile_pool(name="const", bufs=1))
         x2_pool = ctx.enter_context(tc.tile_pool(name="x2", bufs=HALVES))
         x1_pool = ctx.enter_context(tc.tile_pool(name="x1", bufs=3))
-        tree_pool = ctx.enter_context(tc.tile_pool(name="tree", bufs=2))
-        grouped_pool = ctx.enter_context(tc.tile_pool(name="grouped", bufs=3))
-        code_pool = ctx.enter_context(tc.tile_pool(name="codes", bufs=3))
+        small_tree_pool = ctx.enter_context(tc.tile_pool(name="small_trees", bufs=2))
+        large_tree_pool = ctx.enter_context(tc.tile_pool(name="large_trees", bufs=1))
+        r_pool = ctx.enter_context(tc.tile_pool(name="r", bufs=1))
+        x1_grouped_pool = ctx.enter_context(tc.tile_pool(name="x1_grouped", bufs=3))
+        r_grouped_pool = ctx.enter_context(tc.tile_pool(name="r_grouped", bufs=2))
+        x1_code_pool = ctx.enter_context(tc.tile_pool(name="x1_codes", bufs=2))
+        r_code_pool = ctx.enter_context(tc.tile_pool(name="r_codes", bufs=2))
         out_pool = ctx.enter_context(tc.tile_pool(name="outs", bufs=2))
-        pair_pool = ctx.enter_context(tc.tile_pool(name="pair_outs", bufs=4))
+        biased_pool = ctx.enter_context(tc.tile_pool(name="biased", bufs=2))
+        pair_out_pool = ctx.enter_context(tc.tile_pool(name="pair_outs", bufs=4))
         psum_in = ctx.enter_context(tc.psum_pool(name="psum_in", bufs=3))
         psum_acc = ctx.enter_context(tc.psum_pool(name="psum_acc", bufs=3))
         psum_out = ctx.enter_context(tc.psum_pool(name="psum_out", bufs=2))
@@ -67,27 +90,27 @@ def tile_differentiablelogicmachine_pb_t_kernel(tc, x0, x1, x2, W1_words, W1_sca
         x2_tiles = {}
         x1_tiles = {}
 
-        def pieces_of(chunk):
-            count = CHUNKS[chunk][2]
-            size = 1 if chunk == 0 else 2 if chunk < CATCHING_UP else count
-            return [(start, size) for start in range(0, count, size)]
+        def pieces_of(tree):
+            count = TREES[tree][2]
+            size = 1 if tree == 0 else 2 if tree < CATCHING_UP else BATCH
+            return [(start, min(size, count - start)) for start in range(0, count, size)]
 
-        def load_x2(chunk):
-            half, first, count = CHUNKS[chunk]
+        def load_x2(tree):
+            half, first, count = TREES[tree]
             if first == 0:
                 x2_sb = x2_pool.tile([P, RUNS, RUN], BF16)
                 x2_tiles[half] = x2_sb
             table = x2[half * P : (half + 1) * P].rearrange("b i j c -> b (i j c)")
             runs = table[:, C2:].rearrange("b (g r) -> b g r", r=RUN + C2)
-            for start, n in pieces_of(chunk):
+            for start, n in pieces_of(tree):
                 g0, g1 = first + start, min(first + start + n, RUNS)
-                for r0, r1 in RUN_HALVES if chunk == 0 else ((0, RUN),):
+                for r0, r1 in RUN_HALVES if tree == 0 else ((0, RUN),):
                     nc.sync.dma_start(out=x2_tiles[half][:, g0:g1, r0:r1], in_=runs[:, g0:g1, r0:r1])
 
-        def load_x1(chunk):
-            half, first, count = CHUNKS[chunk]
+        def load_x1(batch):
+            half, first, count = place_of(batch)
             x1_sb = x1_pool.tile([P, count, C1], BF16)
-            x1_tiles[chunk] = x1_sb
+            x1_tiles[batch] = x1_sb
             nc.sync.dma_start(out=x1_sb[:], in_=x1[half * P : (half + 1) * P, first : first + count, :])
 
         x0_sb = const.tile([P, HALVES, C0], BF16)
@@ -145,8 +168,10 @@ def tile_differentiablelogicmachine_pb_t_kernel(tc, x0, x1, x2, W1_words, W1_sca
                 )
             nc.sync.dma_start(out=bias_row[:], in_=b1.partition_broadcast(P))
 
+        load_x2(3)
         nc.sync.dma_start(out=bias_rows[0:OUT_HALVES, :], in_=b1.rearrange("(h o) -> h o", h=OUT_HALVES))
         load_weight()
+        load_x1(2)
 
         def transpose_words(bank_part, words, first):
             for u in range(2):
@@ -167,7 +192,8 @@ def tile_differentiablelogicmachine_pb_t_kernel(tc, x0, x1, x2, W1_words, W1_sca
             nc.tensor.transpose(bank[:], bias_rows[:], ident_bf16[:])
             nc.scalar.copy(out=bias[:], in_=bank[:, 0:OUT_HALVES])
 
-        trees = {}
+        tops = {}
+        lows = {}
         r_tiles = {}
         x1_grouped = {}
         r_grouped = {}
@@ -175,52 +201,57 @@ def tile_differentiablelogicmachine_pb_t_kernel(tc, x0, x1, x2, W1_words, W1_sca
         r_mx = {}
         sigmoids = {}
 
-        def partners_of(chunk):
-            half, first, count = CHUNKS[chunk]
+        def partners_of(tree):
+            half, first, count = TREES[tree]
             rows = x2_tiles[half][:].rearrange("b g r -> b (g r)").rearrange("b (i s c) -> b i s c", s=PARTNERS, c=C2)
             return rows[:, first : first + count]
 
-        def start_trees(chunk):
-            count = CHUNKS[chunk][2]
-            top = tree_pool.tile([P, count, 8, C2], BF16)
-            low = tree_pool.tile([P, count, 8, C2], BF16)
-            trees[chunk] = ((ALU.max, top), (ALU.min, low))
-            nc.scalar.activation(out=top[:, :, 7, :], in_=partners_of(chunk)[:, :, 14, :], func=ACT.Relu)
+        def start_tree(tree):
+            count = TREES[tree][2]
+            if count > BATCH:
+                top = large_tree_pool.tile([P, count, 8, C2], BF16)
+            else:
+                top = small_tree_pool.tile([P, count, 8, C2], BF16)
+            tops[tree] = top
+            nc.scalar.activation(out=top[:, :, 7, :], in_=partners_of(tree)[:, :, 14, :], func=ACT.Relu)
 
-        def tree_first_level(chunk):
-            x = partners_of(chunk)
-            for start, n in pieces_of(chunk):
+        def trees_of(tree):
+            return ((ALU.max, tops[tree]), (ALU.min, lows[tree]))
+
+        def first_level(tree):
+            x = partners_of(tree)
+            low = large_tree_pool.tile([P, TREES[tree][2], 8, C2], BF16)
+            lows[tree] = low
+            for start, n in pieces_of(tree):
                 piece = slice(start, start + n)
-                for place, pairs in ((0, 4), (4, 3)) if chunk == 0 else ((0, 7),):
+                for place, pairs in ((0, 4), (4, 3)) if tree == 0 else ((0, 7),):
                     one, other = 2 * place, 2 * place + pairs
-                    for op, t in trees[chunk]:
+                    for op, t in trees_of(tree):
                         nc.vector.tensor_tensor(
                             out=t[:, piece, place : place + pairs, :],
                             in0=x[:, piece, one : one + pairs, :],
                             in1=x[:, piece, other : other + pairs, :],
                             op=op,
                         )
-            low = trees[chunk][1][1]
             nc.vector.tensor_scalar_min(out=low[:, :, 7, :], in0=x[:, :, 14, :], scalar1=1.0)
 
-        def tree_other_levels(chunk, quantise_before_last_level):
-            count = CHUNKS[chunk][2]
-            r = tree_pool.tile([P, count, 2, C2], BF16)
-            r_tiles[chunk] = r
+        def other_levels(tree, quantise_before_last_level):
+            r = r_pool.tile([P, TREES[tree][2], 2, C2], BF16)
+            r_tiles[tree] = r
             for width in (4, 2):
-                for op, t in trees[chunk]:
+                for op, t in trees_of(tree):
                     nc.vector.tensor_tensor(
                         out=t[:, :, 0:width, :], in0=t[:, :, 0:width, :], in1=t[:, :, width : 2 * width, :], op=op
                     )
             quantise_before_last_level()
-            for which, (op, t) in enumerate(trees[chunk]):
+            for which, (op, t) in enumerate(trees_of(tree)):
                 nc.vector.tensor_tensor(out=r[:, :, which, :], in0=t[:, :, 0, :], in1=t[:, :, 1, :], op=op)
 
-        def transpose_x1(chunk):
-            count = CHUNKS[chunk][2]
-            words = x1_tiles[chunk][:].rearrange("b a k -> b (a k)").bitcast(F32)
-            grouped = grouped_pool.tile([P, count, P, 4], BF16, align_bytes=64, tag="x1_grouped")
-            x1_grouped[chunk] = grouped
+        def transpose_x1(batch):
+            count = BATCHES[batch][2]
+            words = x1_tiles[batch][:].rearrange("b a k -> b (a k)").bitcast(F32)
+            grouped = x1_grouped_pool.tile([P, count, P, 4], BF16, align_bytes=64)
+            x1_grouped[batch] = grouped
             for pair in range(count // 2):
                 bank = psum_in.tile([P, 2, 2, P], F32, tag="bank_in")
                 for j in range(2):
@@ -229,20 +260,21 @@ def tile_differentiablelogicmachine_pb_t_kernel(tc, x0, x1, x2, W1_words, W1_sca
                     out=grouped[:, 2 * pair : 2 * pair + 2].bitcast(F32), in_=bank[:].rearrange("p a u b -> p a b u")
                 )
 
-        def transpose_r(chunk):
-            pairs = CHUNKS[chunk][2] // 2
-            words = r_tiles[chunk][:].rearrange("b a m c -> b (a m c)").bitcast(F32)
-            grouped = grouped_pool.tile([P, pairs, P, 4], BF16, align_bytes=64, tag="r_grouped")
-            r_grouped[chunk] = grouped
+        def transpose_r(batch):
+            tree, start, count = BATCHES[batch]
+            pairs = count // 2
+            words = r_tiles[tree][:].rearrange("b a m c -> b (a m c)").bitcast(F32)
+            grouped = r_grouped_pool.tile([P, pairs, P, 4], BF16, align_bytes=64)
+            r_grouped[batch] = grouped
             bank = psum_in.tile([P, pairs, 2, P], F32, tag="bank_in")
             for pair in range(pairs):
-                transpose_words(bank[:, pair], words, pair * 2 * C2)
+                transpose_words(bank[:, pair], words, (start + 2 * pair) * C2)
             nc.scalar.copy(out=grouped[:].bitcast(F32), in_=bank[:].rearrange("p a u b -> p a b u"))
 
-        def quantise(grouped, tag):
+        def quantise(grouped, pool):
             columns = grouped.shape[1]
-            codes = code_pool.tile([P, columns, P], U32, align_bytes=64, tag=tag + "_codes")
-            scales = code_pool.tile([P, columns, P], U8, align_bytes=64, tag=tag + "_scales")
+            codes = pool.tile([P, columns, P], U32, align_bytes=64)
+            scales = pool.tile([P, columns, P], U8, align_bytes=64)
             nc.vector.quantize_mx(
                 out=codes[:].rearrange("p a b -> p (a b)").bitcast(FP8X4),
                 scales=scales[:].rearrange("p a b -> p (a b)"),
@@ -250,33 +282,23 @@ def tile_differentiablelogicmachine_pb_t_kernel(tc, x0, x1, x2, W1_words, W1_sca
             )
             return codes, scales
 
-        def quantise_x1(chunk):
-            x1_mx[chunk] = quantise(x1_grouped[chunk], "x1")
+        def quantise_x1(batch):
+            x1_mx[batch] = quantise(x1_grouped[batch], x1_code_pool)
 
-        def quantise_r(chunk):
-            r_mx[chunk] = quantise(r_grouped[chunk], "r")
+        def quantise_r(batch):
+            r_mx[batch] = quantise(r_grouped[batch], r_code_pool)
 
-        def quantise_for(step):
-            if step == LATE:
-                nc.vector.quantize_mx(
-                    out=x0_codes[:].bitcast(FP8X4), scales=x0_scales[:], in_=x0_grouped[:].rearrange("p b t -> p (b t)")
-                )
-                for chunk in range(LATE - 1):
-                    quantise_x1(chunk)
-                    quantise_r(chunk)
-            if LATE <= step < last:
-                quantise_x1(step - 1)
-            if LATE <= step:
-                quantise_r(step - 1)
-            if step >= last - 1:
-                quantise_x1(step)
+        def quantise_x0():
+            nc.vector.quantize_mx(
+                out=x0_codes[:].bitcast(FP8X4), scales=x0_scales[:], in_=x0_grouped[:].rearrange("p b t -> p (b t)")
+            )
 
-        def multiply(chunk):
-            half, first, count = CHUNKS[chunk]
-            x1_codes, x1_scales = x1_mx[chunk]
-            r_codes, r_scales = r_mx[chunk]
+        def multiply(batch):
+            half, first, count = place_of(batch)
+            x1_codes, x1_scales = x1_mx[batch]
+            r_codes, r_scales = r_mx[batch]
             x0_section = X0_LOW if half == 0 else X0_HIGH
-            sigmoids[chunk] = []
+            sigmoids[batch] = []
             for oh in range(OUT_HALVES):
                 w_cols = slice(2 * P * oh, 2 * P * (oh + 1))
                 s_cols = slice(P * oh, P * (oh + 1))
@@ -313,7 +335,7 @@ def tile_differentiablelogicmachine_pb_t_kernel(tc, x0, x1, x2, W1_words, W1_sca
                     )
                 sig = out_pool.tile([P, count, P], F32, tag="sig")
                 nc.scalar.activation(out=sig[:], in_=acc[:], func=ACT.Sigmoid, bias=bias[:, oh : oh + 1], scale=1.0)
-                sigmoids[chunk].append(sig)
+                sigmoids[batch].append(sig)
 
         pair_accs = {}
 
@@ -328,69 +350,94 @@ def tile_differentiablelogicmachine_pb_t_kernel(tc, x0, x1, x2, W1_words, W1_sca
                 stop=stop,
             )
 
-        def start_pair(chunk):
+        def start_pair(batch):
             acc = psum_acc.tile([P, 2, OUT], F32, tag="acc")
-            pair_accs[chunk] = acc
-            codes, code_scales = x1_mx[chunk]
+            pair_accs[batch] = acc
+            codes, code_scales = x1_mx[batch]
             pair_pass(acc, codes[:, 0, :], code_scales[:, 0, :], X1, S_X1, True, False)
             pair_pass(acc, codes[:, 1, :], code_scales[:, 1, :], X1 - 1, S_X1 - 1, False, False)
             pair_pass(acc, x0_codes[:], x0_scales[:], X0_TWIN, S_X0_TWIN, False, False)
 
-        def add_r(chunk):
-            codes, code_scales = r_mx[chunk]
-            pair_pass(pair_accs[chunk], codes[:, 0, :], code_scales[:, 0, :], R_LOW, S_R, False, True)
+        def add_r(batch):
+            codes, code_scales = r_mx[batch]
+            pair_pass(pair_accs[batch], codes[:, 0, :], code_scales[:, 0, :], R_LOW, S_R, False, True)
 
-        def finish_pair(chunk):
-            half, first, count = CHUNKS[chunk]
+        def finish_pair(batch):
+            half, first, count = place_of(batch)
             for a in range(count):
-                biased = pair_pool.tile([P, OUT], F32, tag="biased")
-                nc.vector.tensor_tensor(out=biased[:], in0=pair_accs[chunk][:, a, :], in1=bias_row[:], op=ALU.add)
-                last_out = pair_pool.tile([P, OUT], F32, tag="last_out")
+                biased = biased_pool.tile([P, OUT], F32)
+                nc.vector.tensor_tensor(out=biased[:], in0=pair_accs[batch][:, a, :], in1=bias_row[:], op=ALU.add)
+                last_out = pair_out_pool.tile([P, OUT], F32)
                 nc.scalar.activation(out=last_out[:], in_=biased[:], func=ACT.Sigmoid)
                 nc.sync.dma_start(out=out[half * P : (half + 1) * P, first + a, :], in_=last_out[:])
 
-        def transpose_back_and_store(chunk):
-            half, first, count = CHUNKS[chunk]
+        def transpose_back_and_store(batch):
+            half, first, count = place_of(batch)
             result = out_pool.tile([P, count, OUT], F32, tag="result")
             for oh in range(OUT_HALVES):
                 back = psum_out.tile([P, count, P], F32, tag="back")
                 for a in range(count):
-                    nc.tensor.transpose(back[:, a, :], sigmoids[chunk][oh][:, a, :], ident_f32[:])
+                    nc.tensor.transpose(back[:, a, :], sigmoids[batch][oh][:, a, :], ident_f32[:])
                 nc.scalar.copy(out=result[:, :, P * oh : P * (oh + 1)], in_=back[:])
             nc.sync.dma_start(out=out[half * P : (half + 1) * P, first : first + count, :], in_=result[:])
 
-        start_trees(0)
-        for step in range(N_CHUNKS):
-            if step + 3 < N_CHUNKS:
-                load_x2(step + 3)
-            if step + 2 < N_CHUNKS:
-                load_x1(step + 2)
-            if step + 2 == last:
+        start_tree(0)
+        for step in range(last_tree + 1):
+            if step + 3 <= last_tree:
+                for batch in batches_of(step + 3):
+                    load_x1(batch)
+            if step + 4 <= last_tree:
+                load_x2(step + 4)
+            if step + 2 == last_tree:
                 load_twins()
-            tree_first_level(step)
-            if step >= 1:
-                transpose_r(step - 1)
+            first_level(step)
+            done = batches_of(step - 1) if step >= 1 else []
+            for batch in done:
+                transpose_r(batch)
+            early, late = done[:-1], done[-1:]
             if step == LATE:
                 transpose_x0()
-                for chunk in range(LATE):
-                    transpose_x1(chunk)
+                for batch in range(LATE):
+                    transpose_x1(batch)
             if step > LATE:
-                transpose_back_and_store(step - 2)
-            if LATE <= step < last - 1:
-                transpose_x1(step)
-            if last - 2 <= step < last:
-                transpose_x1(step + 1)
-            if step < last:
-                start_trees(step + 1)
-            tree_other_levels(step, lambda: quantise_for(step))
+                transpose_back_and_store(done[0] - 1)
+            for batch in early:
+                quantise_x1(batch)
+                quantise_r(batch)
+                multiply(batch)
+            if LATE <= step < last_tree - 1:
+                for batch in batches_of(step):
+                    transpose_x1(batch)
+            if last_tree - 2 <= step < last_tree:
+                transpose_x1(batches_of(step + 1)[0])
+            for batch in early:
+                transpose_back_and_store(batch)
+            if step < last_tree:
+                start_tree(step + 1)
+
+            def quantise_late():
+                if step < LATE:
+                    return
+                if step == LATE:
+                    quantise_x0()
+                    for batch in range(LATE - 1):
+                        quantise_x1(batch)
+                        quantise_r(batch)
+                if step < last_tree:
+                    quantise_x1(late[0])
+                quantise_r(late[0])
+                if step >= last_tree - 1:
+                    quantise_x1(batches_of(step)[0])
+
+            other_levels(step, quantise_late)
             if step == LATE:
                 transpose_bias()
-                for chunk in range(LATE - 1):
-                    multiply(chunk)
-                    transpose_back_and_store(chunk)
-            if LATE <= step < last:
-                multiply(step - 1)
-            if step == last - 1:
+                for batch in range(LATE - 1):
+                    multiply(batch)
+                    transpose_back_and_store(batch)
+            if LATE <= step < last_tree:
+                multiply(late[0])
+            if step == last_tree - 1:
                 start_pair(last - 1)
         add_r(last - 1)
         transpose_r(last)

@@ -339,28 +339,42 @@ def tile_differentiablelogicmachine_pb_t_kernel(tc, x0, x1, x2, W1_words, W1_sca
 
         pair_accs = {}
 
-        def pair_pass(acc, codes, code_scales, section, scale_section, start, stop):
+        def pair_pass(out_cols, codes, code_scales, w, s, start, stop):
             nc.tensor.matmul_mx(
-                out=acc[:].rearrange("p a n -> p (a n)"),
+                out=out_cols,
                 lhsT=codes.bitcast(FP8X4),
                 lhsT_scale=code_scales,
-                rhs=weights[:, section : section + 2, :].rearrange("p s n -> p (s n)").bitcast(FP4X4),
-                rhs_scale=weight_scales[:, scale_section : scale_section + 2, :].rearrange("p s n -> p (s n)"),
+                rhs=w.bitcast(FP4X4),
+                rhs_scale=s,
                 start=start,
                 stop=stop,
+            )
+
+        def two_sections(section, scale_section):
+            return (
+                weights[:, section : section + 2, :].rearrange("p s n -> p (s n)"),
+                weight_scales[:, scale_section : scale_section + 2, :].rearrange("p s n -> p (s n)"),
             )
 
         def start_pair(batch):
             acc = psum_acc.tile([P, 2, OUT], F32, tag="acc")
             pair_accs[batch] = acc
             codes, code_scales = x1_mx[batch]
-            pair_pass(acc, codes[:, 0, :], code_scales[:, 0, :], X1, S_X1, True, False)
-            pair_pass(acc, codes[:, 1, :], code_scales[:, 1, :], X1 - 1, S_X1 - 1, False, False)
-            pair_pass(acc, x0_codes[:], x0_scales[:], X0_TWIN, S_X0_TWIN, False, False)
+            both = acc[:].rearrange("p a n -> p (a n)")
+            w, s = two_sections(X0_TWIN, S_X0_TWIN)
+            pair_pass(both, x0_codes[:], x0_scales[:], w, s, True, False)
+            for a in range(2):
+                for oh in range(OUT_HALVES):
+                    w = weights[:, X1, 2 * P * oh : 2 * P * (oh + 1)]
+                    s = weight_scales[:, S_X1, P * oh : P * (oh + 1)]
+                    cols = acc[:, a, P * oh : P * (oh + 1)]
+                    pair_pass(cols, codes[:, a, :], code_scales[:, a, :], w, s, False, False)
 
         def add_r(batch):
             codes, code_scales = r_mx[batch]
-            pair_pass(pair_accs[batch], codes[:, 0, :], code_scales[:, 0, :], R_LOW, S_R, False, True)
+            w, s = two_sections(R_LOW, S_R)
+            both = pair_accs[batch][:].rearrange("p a n -> p (a n)")
+            pair_pass(both, codes[:, 0, :], code_scales[:, 0, :], w, s, False, True)
 
         def finish_pair(batch):
             half, first, count = place_of(batch)
@@ -383,11 +397,11 @@ def tile_differentiablelogicmachine_pb_t_kernel(tc, x0, x1, x2, W1_words, W1_sca
 
         start_tree(0)
         for step in range(last_tree + 1):
+            if step + 4 <= last_tree:
+                load_x2(step + 4)
             if step + 3 <= last_tree:
                 for batch in batches_of(step + 3):
                     load_x1(batch)
-            if step + 4 <= last_tree:
-                load_x2(step + 4)
             if step + 2 == last_tree:
                 load_twins()
             first_level(step)
@@ -426,8 +440,8 @@ def tile_differentiablelogicmachine_pb_t_kernel(tc, x0, x1, x2, W1_words, W1_sca
                 if step < last_tree:
                     quantise_x1(late[0])
                 quantise_r(late[0])
-                if step >= last_tree - 1:
-                    quantise_x1(batches_of(step)[0])
+                if step == last_tree - 1:
+                    quantise_x1(last - 1)
 
             other_levels(step, quantise_late)
             if step == LATE:
@@ -441,6 +455,7 @@ def tile_differentiablelogicmachine_pb_t_kernel(tc, x0, x1, x2, W1_words, W1_sca
                 start_pair(last - 1)
         add_r(last - 1)
         transpose_r(last)
+        quantise_x1(last)
         start_pair(last)
         finish_pair(last - 1)
         quantise_r(last)

@@ -20,14 +20,14 @@ HALVES = SCENES // P
 PARTNERS = OBJECTS - 1
 RUN = OBJECTS * C2
 RUNS = OBJECTS - 1
-RUN_HALVES = ((0, RUN // 2), (RUN // 2, RUN))
+RUN_PARTS = ((0, RUN // 2), (RUN // 2, RUN))
 OUT_HALVES = OUT // P
 TREE_SIZES = ((2, 2, 4, 8), (8, 4, 2, 2))
 BATCH = 4
 CATCHING_UP = 3
-X0_LOW, X0_TWIN, X0_HIGH, X1, R_LOW, R_HIGH, N_SECTIONS = 0, 1, 2, 4, 6, 7, 8
-S_X0_TWIN, S_X0, S_X1, S_R, S_R_TWIN, N_SCALE_SECTIONS = 0, 1, 2, 4, 5, 6
 LATE = 2
+X0_LOW, X0_TWIN, X0_HIGH, X1, R_LOW, R_HIGH, N_SECTIONS = 0, 1, 2, 3, 4, 5, 6
+S_X0_TWIN, S_X0, S_X1, S_UNUSED, S_R, S_R_TWIN, N_SCALE_SECTIONS = 0, 1, 2, 3, 4, 5, 6
 
 FLOPS = 2 * SCENES * OBJECTS * K * OUT
 BYTES = (
@@ -104,7 +104,7 @@ def tile_differentiablelogicmachine_pb_t_kernel(tc, x0, x1, x2, W1_words, W1_sca
             runs = table[:, C2:].rearrange("b (g r) -> b g r", r=RUN + C2)
             for start, n in pieces_of(tree):
                 g0, g1 = first + start, min(first + start + n, RUNS)
-                for r0, r1 in RUN_HALVES if tree == 0 else ((0, RUN),):
+                for r0, r1 in RUN_PARTS if tree == 0 else ((0, RUN),):
                     nc.sync.dma_start(out=x2_tiles[half][:, g0:g1, r0:r1], in_=runs[:, g0:g1, r0:r1])
 
         def load_x1(batch):

from contextlib import ExitStack

import concourse.mybir as mybir
from concourse.masks import make_identity

BF16 = mybir.dt.bfloat16
F32 = mybir.dt.float32
I32 = mybir.dt.int32
U8 = mybir.dt.uint8
U32 = mybir.dt.uint32
FP8X4 = mybir.dt.float8_e4m3fn_x4
FP4X4 = mybir.dt.float4_e2m1fn_x4
ALU = mybir.AluOpType
ACT = mybir.ActivationFunctionType

P = 128
SCENES, OBJECTS, C0, C1, C2, OUT = 256, 16, 256, 512, 128, 256
K = C0 + C1 + 2 * C2
HALVES = SCENES // P
PARTNERS = OBJECTS - 1
RUN = OBJECTS * C2
RUNS = OBJECTS - 1
RUN_PARTS = ((0, RUN // 2), (RUN // 2, RUN))
OUT_HALVES = OUT // P
TREE_SIZES = ((2, 2, 4, 8), (8, 4, 2, 2))
BATCH = 4
CATCHING_UP = 3
LATE = 2
X0_LOW, X0_TWIN, X0_HIGH, X1, R_LOW, R_HIGH, N_SECTIONS = 0, 1, 2, 3, 4, 5, 6
S_X0_TWIN, S_X0, S_X1, S_UNUSED, S_R, S_R_TWIN, N_SCALE_SECTIONS = 0, 1, 2, 3, 4, 5, 6

FLOPS = 2 * SCENES * OBJECTS * K * OUT
BYTES = (
    2 * (SCENES * C0 + SCENES * OBJECTS * C1 + SCENES * OBJECTS * PARTNERS * C2 + OUT)
    + K * OUT // 2
    + K * OUT // 32
    + 4 * SCENES * OBJECTS * OUT
)


def tree_list():
    trees = []
    for half, sizes in enumerate(TREE_SIZES):
        for n, count in enumerate(sizes):
            trees.append((half, sum(sizes[:n]), count))
    return trees


def batch_list(trees):
    batches = []
    for tree, (half, first, count) in enumerate(trees):
        for start in range(0, count, BATCH):
            batches.append((tree, start, min(BATCH, count - start)))
    return batches


def tile_differentiablelogicmachine_pb_t_kernel(tc, x0, x1, x2, W1_words, W1_scales, b1, out):
    nc = tc.nc
    TREES = tree_list()
    BATCHES = batch_list(TREES)
    last_tree = len(TREES) - 1
    last = len(BATCHES) - 1

    def batches_of(tree):
        return [batch for batch, (owner, start, count) in enumerate(BATCHES) if owner == tree]

    def place_of(batch):
        tree, start, count = BATCHES[batch]
        return TREES[tree][0], TREES[tree][1] + start, count

    with ExitStack() as ctx:
        const = ctx.enter_context(tc.tile_pool(name="const", bufs=1))
        x2_pool = ctx.enter_context(tc.tile_pool(name="x2", bufs=HALVES))
        x1_pool = ctx.enter_context(tc.tile_pool(name="x1", bufs=3))
        small_tree_pool = ctx.enter_context(tc.tile_pool(name="small_trees", bufs=2))
        large_tree_pool = ctx.enter_context(tc.tile_pool(name="large_trees", bufs=1))
        r_pool = ctx.enter_context(tc.tile_pool(name="r", bufs=1))
        x1_grouped_pool = ctx.enter_context(tc.tile_pool(name="x1_grouped", bufs=3))
        r_grouped_pool = ctx.enter_context(tc.tile_pool(name="r_grouped", bufs=2))
        x1_code_pool = ctx.enter_context(tc.tile_pool(name="x1_codes", bufs=2))
        r_code_pool = ctx.enter_context(tc.tile_pool(name="r_codes", bufs=2))
        out_pool = ctx.enter_context(tc.tile_pool(name="outs", bufs=2))
        biased_pool = ctx.enter_context(tc.tile_pool(name="biased", bufs=2))
        pair_out_pool = ctx.enter_context(tc.tile_pool(name="pair_outs", bufs=4))
        psum_in = ctx.enter_context(tc.psum_pool(name="psum_in", bufs=3))
        psum_acc = ctx.enter_context(tc.psum_pool(name="psum_acc", bufs=3))
        psum_out = ctx.enter_context(tc.psum_pool(name="psum_out", bufs=2))
        ctx.enter_context(tc.manual_schedule())

        x2_tiles = {}
        x1_tiles = {}

        def pieces_of(tree):
            count = TREES[tree][2]
            size = 1 if tree == 0 else 2 if tree < CATCHING_UP else BATCH
            return [(start, min(size, count - start)) for start in range(0, count, size)]

        def load_x2(tree):
            half, first, count = TREES[tree]
            if first == 0:
                x2_sb = x2_pool.tile([P, RUNS, RUN], BF16)
                x2_tiles[half] = x2_sb
            table = x2[half * P : (half + 1) * P].rearrange("b i j c -> b (i j c)")
            runs = table[:, C2:].rearrange("b (g r) -> b g r", r=RUN + C2)
            for start, n in pieces_of(tree):
                g0, g1 = first + start, min(first + start + n, RUNS)
                for r0, r1 in RUN_PARTS if tree == 0 else ((0, RUN),):
                    nc.sync.dma_start(out=x2_tiles[half][:, g0:g1, r0:r1], in_=runs[:, g0:g1, r0:r1])

        def load_x1(batch):
            half, first, count = place_of(batch)
            x1_sb = x1_pool.tile([P, count, C1], BF16)
            x1_tiles[batch] = x1_sb
            nc.sync.dma_start(out=x1_sb[:], in_=x1[half * P : (half + 1) * P, first : first + count, :])

        x0_sb = const.tile([P, HALVES, C0], BF16)
        bias_rows = const.tile([P, P], BF16)
        nc.vector.memset(bias_rows[:], 0.0)
        load_x2(0)
        load_x2(1)
        load_x2(2)
        load_x1(0)
        nc.sync.dma_start(out=x0_sb[:], in_=x0.rearrange("(h b) k -> b h k", h=HALVES))
        load_x1(1)

        weights = const.tile([P, N_SECTIONS, 2 * OUT], U8, align_bytes=64)
        weight_scales = const.tile([P, N_SCALE_SECTIONS, OUT], U8, align_bytes=64)
        nc.vector.memset(weights[:, 0:X1].bitcast(I32), 0)
        nc.vector.memset(weights[:, X1 + 1 :].bitcast(I32), 0)
        nc.vector.memset(weight_scales[:].bitcast(I32), 0)
        table_warmer = const.tile([P, 2], F32)
        nc.vector.memset(table_warmer[:, 0:1], 0.0)
        nc.scalar.activation(out=table_warmer[:, 1:2], in_=table_warmer[:, 0:1], func=ACT.Sigmoid)

        ident_f32 = const.tile([P, P], F32)
        make_identity(nc, ident_f32[:])
        ident_bf16 = const.tile([P, P], BF16)
        make_identity(nc, ident_bf16[:])

        words_by_64 = W1_words.rearrange("g (s p) n -> p (g s) n", p=64)
        x0_and_r = words_by_64[:, 0:4:3, :].bitcast(I32)
        scales_by_8 = W1_scales.rearrange("g (s q) n -> q (g s) n", q=8)

        bias_row = const.tile([P, OUT], BF16)

        def load_weight():
            nc.sync.dma_start(
                out=weights[:, X1].bitcast(I32), in_=W1_words.rearrange("g p n -> (g p) n")[64:192, :].bitcast(I32)
            )
            nc.sync.dma_start(out=weights[0:64, X0_LOW : R_LOW + 1 : R_LOW - X0_LOW].bitcast(I32), in_=x0_and_r)
            nc.sync.dma_start(out=weights[64:128, X0_HIGH : R_HIGH + 1 : R_HIGH - X0_HIGH].bitcast(I32), in_=x0_and_r)
            for quad in range(4):
                rows = scales_by_8[4 * (quad % 2) : 4 * (quad % 2) + 4].bitcast(I32)
                plane = weight_scales[32 * quad : 32 * quad + 4]
                if quad < 2:
                    nc.sync.dma_start(out=plane[:, S_X0 : S_R + 1].bitcast(I32), in_=rows)
                else:
                    nc.sync.dma_start(out=plane[:, S_X0 : S_R + 1 : S_R - S_X0].bitcast(I32), in_=rows[:, 0:4:3])
                    nc.sync.dma_start(out=plane[:, S_X1].bitcast(I32), in_=rows[:, 2])

        def load_twins():
            nc.sync.dma_start(out=weights[64:128, X0_TWIN].bitcast(I32), in_=words_by_64[:, 0, :].bitcast(I32))
            for quad in range(2, 4):
                rows = scales_by_8[4 * (quad % 2) : 4 * (quad % 2) + 4].bitcast(I32)
                plane = weight_scales[32 * quad : 32 * quad + 4]
                nc.sync.dma_start(
                    out=plane[:, S_X0_TWIN : S_R_TWIN + 1 : S_R_TWIN - S_X0_TWIN].bitcast(I32), in_=rows[:, 0:4:3]
                )
            nc.sync.dma_start(out=bias_row[:], in_=b1.partition_broadcast(P))

        load_x2(3)
        nc.sync.dma_start(out=bias_rows[0:OUT_HALVES, :], in_=b1.rearrange("(h o) -> h o", h=OUT_HALVES))
        load_weight()
        load_x1(2)

        def transpose_words(bank_part, words, first):
            for u in range(2):
                nc.tensor.transpose(bank_part[:, u, :], words[:, first + u : first + 2 * P : 2], ident_f32[:])

        x0_grouped = const.tile([P, P, 4], BF16, align_bytes=64)
        x0_codes = const.tile([P, P], U32, align_bytes=64)
        x0_scales = const.tile([P, P], U8, align_bytes=64)
        bias = const.tile([P, OUT_HALVES], F32)

        def transpose_x0():
            bank = psum_in.tile([P, 2, P], F32, tag="bank_in")
            transpose_words(bank, x0_sb[:].rearrange("b h k -> b (h k)").bitcast(F32), 0)
            nc.scalar.copy(out=x0_grouped[:].bitcast(F32), in_=bank[:].rearrange("p u b -> p b u"))

        def transpose_bias():
            bank = psum_in.tile([P, P], BF16, tag="bank_in")
            nc.tensor.transpose(bank[:], bias_rows[:], ident_bf16[:])
            nc.scalar.copy(out=bias[:], in_=bank[:, 0:OUT_HALVES])

        tops = {}
        lows = {}
        r_tiles = {}
        x1_grouped = {}
        r_grouped = {}
        x1_mx = {}
        r_mx = {}
        sigmoids = {}

        def partners_of(tree):
            half, first, count = TREES[tree]
            rows = x2_tiles[half][:].rearrange("b g r -> b (g r)").rearrange("b (i s c) -> b i s c", s=PARTNERS, c=C2)
            return rows[:, first : first + count]

        def start_tree(tree):
            count = TREES[tree][2]
            if count > BATCH:
                top = large_tree_pool.tile([P, count, 8, C2], BF16)
            else:
                top = small_tree_pool.tile([P, count, 8, C2], BF16)
            tops[tree] = top
            nc.scalar.activation(out=top[:, :, 7, :], in_=partners_of(tree)[:, :, 14, :], func=ACT.Relu)

        def trees_of(tree):
            return ((ALU.max, tops[tree]), (ALU.min, lows[tree]))

        def first_level(tree):
            x = partners_of(tree)
            low = large_tree_pool.tile([P, TREES[tree][2], 8, C2], BF16)
            lows[tree] = low
            for start, n in pieces_of(tree):
                piece = slice(start, start + n)
                for place, pairs in ((0, 4), (4, 3)) if tree == 0 else ((0, 7),):
                    one, other = 2 * place, 2 * place + pairs
                    for op, t in trees_of(tree):
                        nc.vector.tensor_tensor(
                            out=t[:, piece, place : place + pairs, :],
                            in0=x[:, piece, one : one + pairs, :],
                            in1=x[:, piece, other : other + pairs, :],
                            op=op,
                        )
            nc.vector.tensor_scalar_min(out=low[:, :, 7, :], in0=x[:, :, 14, :], scalar1=1.0)

        def other_levels(tree, quantise_before_last_level):
            r = r_pool.tile([P, TREES[tree][2], 2, C2], BF16)
            r_tiles[tree] = r
            for width in (4, 2):
                for op, t in trees_of(tree):
                    nc.vector.tensor_tensor(
                        out=t[:, :, 0:width, :], in0=t[:, :, 0:width, :], in1=t[:, :, width : 2 * width, :], op=op
                    )
            quantise_before_last_level()
            for which, (op, t) in enumerate(trees_of(tree)):
                nc.vector.tensor_tensor(out=r[:, :, which, :], in0=t[:, :, 0, :], in1=t[:, :, 1, :], op=op)

        def transpose_x1(batch):
            count = BATCHES[batch][2]
            words = x1_tiles[batch][:].rearrange("b a k -> b (a k)").bitcast(F32)
            grouped = x1_grouped_pool.tile([P, count, P, 4], BF16, align_bytes=64)
            x1_grouped[batch] = grouped
            for pair in range(count // 2):
                bank = psum_in.tile([P, 2, 2, P], F32, tag="bank_in")
                for j in range(2):
                    transpose_words(bank[:, j], words, (2 * pair + j) * (C1 // 2))
                nc.scalar.copy(
                    out=grouped[:, 2 * pair : 2 * pair + 2].bitcast(F32), in_=bank[:].rearrange("p a u b -> p a b u")
                )

        def transpose_r(batch):
            tree, start, count = BATCHES[batch]
            pairs = count // 2
            words = r_tiles[tree][:].rearrange("b a m c -> b (a m c)").bitcast(F32)
            grouped = r_grouped_pool.tile([P, pairs, P, 4], BF16, align_bytes=64)
            r_grouped[batch] = grouped
            bank = psum_in.tile([P, pairs, 2, P], F32, tag="bank_in")
            for pair in range(pairs):
                transpose_words(bank[:, pair], words, (start + 2 * pair) * C2)
            nc.scalar.copy(out=grouped[:].bitcast(F32), in_=bank[:].rearrange("p a u b -> p a b u"))

        def quantise(grouped, pool):
            columns = grouped.shape[1]
            codes = pool.tile([P, columns, P], U32, align_bytes=64)
            scales = pool.tile([P, columns, P], U8, align_bytes=64)
            nc.vector.quantize_mx(
                out=codes[:].rearrange("p a b -> p (a b)").bitcast(FP8X4),
                scales=scales[:].rearrange("p a b -> p (a b)"),
                in_=grouped[:].rearrange("p a b t -> p (a b t)"),
            )
            return codes, scales

        def quantise_x1(batch):
            x1_mx[batch] = quantise(x1_grouped[batch], x1_code_pool)

        def quantise_r(batch):
            r_mx[batch] = quantise(r_grouped[batch], r_code_pool)

        def quantise_x0():
            nc.vector.quantize_mx(
                out=x0_codes[:].bitcast(FP8X4), scales=x0_scales[:], in_=x0_grouped[:].rearrange("p b t -> p (b t)")
            )

        def multiply(batch):
            half, first, count = place_of(batch)
            x1_codes, x1_scales = x1_mx[batch]
            r_codes, r_scales = r_mx[batch]
            x0_section = X0_LOW if half == 0 else X0_HIGH
            sigmoids[batch] = []
            for oh in range(OUT_HALVES):
                w_cols = slice(2 * P * oh, 2 * P * (oh + 1))
                s_cols = slice(P * oh, P * (oh + 1))
                acc = psum_acc.tile([P, count, P], F32, tag="acc")
                for a in range(count):
                    pair, second = divmod(a, 2)
                    r_section = R_LOW if second == 0 else R_HIGH
                    nc.tensor.matmul_mx(
                        out=acc[:, a, :],
                        lhsT=weights[:, X1, w_cols].bitcast(FP4X4),
                        lhsT_scale=weight_scales[:, S_X1, s_cols],
                        rhs=x1_codes[:, a, :].bitcast(FP8X4),
                        rhs_scale=x1_scales[:, a, :],
                        start=True,
                        stop=False,
                    )
                    nc.tensor.matmul_mx(
                        out=acc[:, a, :],
                        lhsT=weights[:, x0_section, w_cols].bitcast(FP4X4),
                        lhsT_scale=weight_scales[:, S_X0, s_cols],
                        rhs=x0_codes[:].bitcast(FP8X4),
                        rhs_scale=x0_scales[:],
                        start=False,
                        stop=False,
                    )
                    nc.tensor.matmul_mx(
                        out=acc[:, a, :],
                        lhsT=weights[:, r_section, w_cols].bitcast(FP4X4),
                        lhsT_scale=weight_scales[:, S_R, s_cols],
                        rhs=r_codes[:, pair, :].bitcast(FP8X4),
                        rhs_scale=r_scales[:, pair, :],
                        start=False,
                        stop=True,
                    )
                sig = out_pool.tile([P, count, P], F32, tag="sig")
                nc.scalar.activation(out=sig[:], in_=acc[:], func=ACT.Sigmoid, bias=bias[:, oh : oh + 1], scale=1.0)
                sigmoids[batch].append(sig)

        pair_accs = {}

        def pair_pass(out_cols, codes, code_scales, w, s, start, stop):
            nc.tensor.matmul_mx(
                out=out_cols,
                lhsT=codes.bitcast(FP8X4),
                lhsT_scale=code_scales,
                rhs=w.bitcast(FP4X4),
                rhs_scale=s,
                start=start,
                stop=stop,
            )

        def two_sections(section, scale_section):
            return (
                weights[:, section : section + 2, :].rearrange("p s n -> p (s n)"),
                weight_scales[:, scale_section : scale_section + 2, :].rearrange("p s n -> p (s n)"),
            )

        def start_pair(batch):
            acc = psum_acc.tile([P, 2, OUT], F32, tag="acc")
            pair_accs[batch] = acc
            codes, code_scales = x1_mx[batch]
            both = acc[:].rearrange("p a n -> p (a n)")
            w, s = two_sections(X0_TWIN, S_X0_TWIN)
            pair_pass(both, x0_codes[:], x0_scales[:], w, s, True, False)
            for a in range(2):
                for oh in range(OUT_HALVES):
                    w = weights[:, X1, 2 * P * oh : 2 * P * (oh + 1)]
                    s = weight_scales[:, S_X1, P * oh : P * (oh + 1)]
                    cols = acc[:, a, P * oh : P * (oh + 1)]
                    pair_pass(cols, codes[:, a, :], code_scales[:, a, :], w, s, False, False)

        def add_r(batch):
            codes, code_scales = r_mx[batch]
            w, s = two_sections(R_LOW, S_R)
            both = pair_accs[batch][:].rearrange("p a n -> p (a n)")
            pair_pass(both, codes[:, 0, :], code_scales[:, 0, :], w, s, False, True)

        def finish_pair(batch):
            half, first, count = place_of(batch)
            for a in range(count):
                biased = biased_pool.tile([P, OUT], F32)
                nc.vector.tensor_tensor(out=biased[:], in0=pair_accs[batch][:, a, :], in1=bias_row[:], op=ALU.add)
                last_out = pair_out_pool.tile([P, OUT], F32)
                nc.scalar.activation(out=last_out[:], in_=biased[:], func=ACT.Sigmoid)
                nc.sync.dma_start(out=out[half * P : (half + 1) * P, first + a, :], in_=last_out[:])

        def transpose_back_and_store(batch):
            half, first, count = place_of(batch)
            result = out_pool.tile([P, count, OUT], F32, tag="result")
            for oh in range(OUT_HALVES):
                back = psum_out.tile([P, count, P], F32, tag="back")
                for a in range(count):
                    nc.tensor.transpose(back[:, a, :], sigmoids[batch][oh][:, a, :], ident_f32[:])
                nc.scalar.copy(out=result[:, :, P * oh : P * (oh + 1)], in_=back[:])
            nc.sync.dma_start(out=out[half * P : (half + 1) * P, first : first + count, :], in_=result[:])

        start_tree(0)
        for step in range(last_tree + 1):
            if step + 4 <= last_tree:
                load_x2(step + 4)
            if step + 3 <= last_tree:
                for batch in batches_of(step + 3):
                    load_x1(batch)
            if step + 2 == last_tree:
                load_twins()
            first_level(step)
            done = batches_of(step - 1) if step >= 1 else []
            for batch in done:
                transpose_r(batch)
            early, late = done[:-1], done[-1:]
            if step == LATE:
                transpose_x0()
                for batch in range(LATE):
                    transpose_x1(batch)
            if step > LATE:
                transpose_back_and_store(done[0] - 1)
            for batch in early:
                quantise_x1(batch)
                quantise_r(batch)
                multiply(batch)
            if LATE <= step < last_tree - 1:
                for batch in batches_of(step):
                    transpose_x1(batch)
            if last_tree - 2 <= step < last_tree:
                transpose_x1(batches_of(step + 1)[0])
            for batch in early:
                transpose_back_and_store(batch)
            if step < last_tree:
                start_tree(step + 1)

            def quantise_late():
                if step < LATE:
                    return
                if step == LATE:
                    quantise_x0()
                    for batch in range(LATE - 1):
                        quantise_x1(batch)
                        quantise_r(batch)
                if step < last_tree:
                    quantise_x1(late[0])
                quantise_r(late[0])
                if step == last_tree - 1:
                    quantise_x1(last - 1)

            other_levels(step, quantise_late)
            if step == LATE:
                transpose_bias()
                for batch in range(LATE - 1):
                    multiply(batch)
                    transpose_back_and_store(batch)
            if LATE <= step < last_tree:
                multiply(late[0])
            if step == last_tree - 1:
                start_pair(last - 1)
        add_r(last - 1)
        transpose_r(last)
        quantise_x1(last)
        start_pair(last)
        finish_pair(last - 1)
        quantise_r(last)
        add_r(last)
        finish_pair(last)
